import numpy as np
import ml_dtypes


def mxq(x, axis, fmt="e4m3"):
    dtype, down = {"e4m3": (ml_dtypes.float8_e4m3fn, 7), "e5m2": (ml_dtypes.float8_e5m2, 14)}[fmt]
    v = np.moveaxis(np.asarray(x, np.float32).astype(ml_dtypes.bfloat16).astype(np.float64), axis, -1)
    blocks = v.reshape(v.shape[:-1] + (-1, 32))
    amax = np.abs(blocks).max(-1, keepdims=True)
    byte = np.maximum(np.where(amax > 0, np.frexp(amax)[1] - 1 + 127, 0) - down, 1)
    scale = np.exp2(byte - 127.0)
    codes = (blocks / scale).astype(np.float32).astype(dtype).astype(np.float64)
    return np.moveaxis((codes * scale).reshape(v.shape), -1, axis)


WIDE = False


def mx_kscale(k):
    if not WIDE:
        return np.ones(k)
    levels = np.array([10, -10, 5, -5, 0])
    if k % 512:
        return np.exp2(np.random.permutation(np.resize(levels, k // 32))).repeat(32)
    a = np.empty((k // 512, 16))
    for p in range(k // 512):
        a[p, :8] = np.random.permutation(np.resize(levels, 8))
        for g in range(8):
            far = levels[np.abs(levels - a[p, g]) >= 10]
            a[p, g + 8] = far[np.random.randint(len(far))]
    return np.exp2(a.ravel()).repeat(32)


BF16 = ml_dtypes.bfloat16


def bf(x):
    return np.asarray(x, np.float32).astype(BF16)


def f64(x):
    return np.asarray(x).astype(np.float64)


N, IN_F, J, K = 256, 2048, 128, 16


def draw0():
    s = mx_kscale(IN_F)
    s = s / s.max()
    return {"tensor": bf(np.random.standard_normal((N, IN_F)) * s),
            "T": bf(np.random.standard_normal((IN_F, J, K)) * 4.0 / (K * np.sqrt(IN_F)) / s[:, None, None])}


def core(tensor, T):
    x = f64(tensor).reshape(tensor.shape[0], -1)
    feats = (mxq(x, 1, "e4m3") @ mxq(f64(T).reshape(IN_F, J * K), 0, "e4m3")).reshape(N, J, K)
    diversity = np.stack([np.exp(-np.abs(feats[n][None, :, :] - feats).sum(axis=2)).sum(axis=0) for n in range(N)])
    return np.concatenate((x, diversity), axis=1)


def e4m3fn_bytes(y):
    return np.clip(np.asarray(y, np.float64), -448.0, 448.0).astype(np.float32).astype(ml_dtypes.float8_e4m3fn).view(np.uint8)


def e4m3fn_values(b):
    return np.asarray(b, np.uint8).view(ml_dtypes.float8_e4m3fn).astype(np.float64)


def setup_inputs():
    d = draw0()
    x0 = np.asarray(d['T']).astype(np.float64)
    s = (np.max(np.abs(x0), axis=(1, 2), keepdims=True) / 448.0).astype(np.float32)
    out = {}
    for k, v in d.items():
        if k == 'T':
            out['T_bytes'] = e4m3fn_bytes(x0 / s.astype(np.float64))
            out['T_scale'] = s
        else:
            out[k] = v
    return out


def reference(tensor, T_bytes, T_scale):
    return core(tensor, e4m3fn_values(T_bytes) * T_scale.astype(np.float64))

@@ -1,0 +1,418 @@
+from contextlib import ExitStack
+
+import concourse.mybir as mybir
+from concourse.masks import make_identity
+
+FLOPS = 2 * 256 * 2048 * 2048
+
+F32 = mybir.dt.float32
+BF16 = mybir.dt.bfloat16
+U32 = mybir.dt.uint32
+U8 = mybir.dt.uint8
+FP8 = mybir.dt.float8_e4m3fn
+FP8X4 = mybir.dt.float8_e4m3fn_x4
+ALU = mybir.AluOpType
+ACT = mybir.ActivationFunctionType
+AX = mybir.AxisListType
+
+P = 128
+ROWS = 256
+IN_F = 2048
+PACK = 4
+PASSES = IN_F // (P * PACK)
+KK = 16
+PAIRS = KK // 2
+RING = 4
+GROUP = 4
+BATCH = 16
+CHUNK = 384
+GPSIMD_ROWS = 20
+SPLIT = 116
+EXP_LAG = 2
+BIG = 3.0e38
+
+
+def cut_into_chunks(first_rows):
+    chunks = []
+    segments = []
+    used = 0
+    for m0 in first_rows:
+        width = ROWS - m0
+        for r in range(GROUP):
+            c = 0
+            while c < width:
+                take = min(width - c, CHUNK - used)
+                segments.append((m0, r, c, c + take, used))
+                used += take
+                c += take
+                if used == CHUNK:
+                    chunks.append(segments)
+                    segments = []
+                    used = 0
+    if used:
+        chunks.append(segments)
+    return chunks
+
+
+def columns_used(chunk):
+    return chunk[-1][4] + chunk[-1][3] - chunk[-1][2]
+
+
+def tiles_of(chunk):
+    return (columns_used(chunk) + P - 1) // P
+
+
+def filled_up(chunk):
+    spare = tiles_of(chunk) * P - columns_used(chunk)
+    if spare:
+        return chunk + [(0, 0, 0, spare, columns_used(chunk))]
+    return chunk
+
+
+def tile_minibatchdiscriminator_kernel(tc, tensor, T_bytes, T_scale, out):
+    nc = tc.nc
+    with ExitStack() as ctx:
+        keep = ctx.enter_context(tc.tile_pool(name="keep", bufs=1))
+        psum = ctx.enter_context(tc.psum_pool(name="psum", bufs=1))
+
+        warm = keep.tile([P, 2], F32, name="warm")
+        nc.vector.memset(warm[:], 0.0)
+        nc.scalar.activation(out=warm[:, 1:2], in_=warm[:, 0:1], func=ACT.Exp)
+
+        ident = keep.tile([P, P], F32, name="ident")
+        make_identity(nc, ident[:])
+        col_sums = keep.tile([P, GROUP, ROWS], F32, name="col_sums")
+        nc.gpsimd.memset(col_sums[:], 0.0)
+        row_sums = keep.tile([P, ROWS], F32, name="row_sums")
+        row_sums2 = keep.tile([P, ROWS], F32, name="row_sums2")
+        nc.gpsimd.memset(row_sums2[:], 0.0)
+
+        f_sb = keep.tile([P, KK, ROWS], F32, name="f_sb")
+        f_bank = []
+
+        with ExitStack() as head:
+            bytes_pool = head.enter_context(tc.tile_pool(name="bytes_pool", bufs=1))
+            stage = head.enter_context(tc.tile_pool(name="stage", bufs=2))
+            mxp = head.enter_context(tc.tile_pool(name="mxp", bufs=1))
+
+            x_sb = mxp.tile([P, 2, IN_F], BF16, name="x_sb")
+            nc.sync.dma_start(out=x_sb[:], in_=tensor.rearrange("(h p) i -> p h i", p=P))
+            t_scale = mxp.tile([P, PASSES, PACK], F32, name="t_scale")
+            nc.scalar.dma_start(out=t_scale[:], in_=T_scale.rearrange("(g p t) a b -> p g (t a b)", p=P, t=PACK))
+            bytes_view = T_bytes.rearrange("(g p t) j k -> g p (t j k)", p=P, t=PACK)
+            t_bytes = []
+            for g in range(PASSES):
+                tb = bytes_pool.tile([P, PACK * IN_F], U8, name="t_bytes%d" % g)
+                for piece in range(2):
+                    run = slice(piece * 4096, (piece + 1) * 4096)
+                    nc.sync.dma_start(out=tb[:, run], in_=bytes_view[g][:, run])
+                t_bytes.append(tb)
+
+            x_f32 = mxp.tile([P, 2, IN_F], F32, name="x_f32")
+            out_x = out[:, 0:IN_F].rearrange("(h p) i -> p h i", p=P)
+            x_grouped = mxp.tile([P, PASSES, ROWS * PACK], BF16, name="x_grouped", align_bytes=64)
+            x_codes = mxp.tile([P, PASSES * ROWS], U32, name="x_codes", align_bytes=64)
+            x_scales = mxp.tile([P, PASSES * ROWS], U8, name="x_scales", align_bytes=64)
+            t_codes = mxp.tile([P, PASSES, IN_F], U32, name="t_codes", align_bytes=64)
+            t_scales = mxp.tile([P, PASSES, IN_F], U8, name="t_scales", align_bytes=64)
+            widened = {}
+
+            def widen(g):
+                w = stage.tile([P, PACK, IN_F], BF16, name="w", tag="w")
+                widened[g] = w
+                for t in range(PACK):
+                    nc.vector.tensor_scalar(out=w[:, t, :], in0=t_bytes[g][:, t * IN_F:(t + 1) * IN_F].bitcast(FP8),
+                                            scalar1=t_scale[:, g, t:t + 1], scalar2=None, op0=ALU.mult)
+
+            def interleave(g, parity, grouped, j0, j1, on_scalar):
+                dst = grouped[:].rearrange("p (c j t) -> p c j t", c=PAIRS, t=PACK)[:, :, j0:j1, :]
+                src = widened[g][:].rearrange("p t (j k) -> p k j t", k=KK)[:, parity:KK:2, j0:j1, :]
+                if on_scalar:
+                    nc.scalar.copy(out=dst, in_=src)
+                else:
+                    nc.vector.tensor_copy(out=dst, in_=src)
+
+            def multiply(g, parity):
+                for q in range(PAIRS):
+                    cols = slice((PAIRS * parity + q) * P, (PAIRS * parity + q + 1) * P)
+                    x_cols = slice(g * ROWS, (g + 1) * ROWS)
+                    nc.tensor.matmul_mx(
+                        out=f_bank[q][:, parity, :],
+                        lhsT=t_codes[:, g, cols].bitcast(FP8X4),
+                        lhsT_scale=t_scales[:, g, cols],
+                        rhs=x_codes[:, x_cols].bitcast(FP8X4),
+                        rhs_scale=x_scales[:, x_cols],
+                        start=(g == 0),
+                        stop=(g == PASSES - 1),
+                    )
+
+            with tc.manual_schedule():
+                for g in range(PASSES):
+                    x_t = psum.tile([P, 2, 2, P], F32, name="x_t%d" % g, tag="bank%d" % g)
+                    for h in range(2):
+                        words = x_sb[:, h, :].bitcast(F32)
+                        for u in range(2):
+                            nc.tensor.transpose(x_t[:, h, u, :], words[:, 256 * g + u:256 * (g + 1):2], ident[:])
+                    nc.vector.tensor_copy(
+                        out=x_grouped[:, g, :].bitcast(F32).rearrange("p (h r u) -> p h r u", h=2, u=2),
+                        in_=x_t[:].rearrange("p h u r -> p h r u"),
+                    )
+                for h in range(2):
+                    nc.scalar.copy(out=x_f32[:, h, :], in_=x_sb[:, h, :])
+                    nc.sync.dma_start(out=out_x[:, h, :], in_=x_f32[:, h, :])
+                widen(0)
+                nc.vector.quantize_mx(out=x_codes[:].bitcast(FP8X4), scales=x_scales[:],
+                                      in_=x_grouped[:].rearrange("p g c -> p (g c)"))
+                widen(1)
+                for q in range(PAIRS):
+                    bank = psum.tile([P, 2, ROWS], F32, name="f_bank%d" % q, tag="bank%d" % q)
+                    f_bank.append(bank)
+                for g in range(PASSES):
+                    last = g == PASSES - 1
+                    grouped = []
+                    for parity in range(2):
+                        t_grouped = stage.tile([P, PAIRS * P * PACK], BF16, name="t_grouped", tag="t_grouped", bufs=4,
+                                               align_bytes=64)
+                        grouped.append(t_grouped)
+                    if last:
+                        interleave(g, 0, grouped[0], P // 2, P, True)
+                        interleave(g, 0, grouped[0], 0, P // 2, False)
+                    else:
+                        interleave(g, 0, grouped[0], 0, P, False)
+                    interleave(g, 1, grouped[1], 0, P, True)
+                    for parity in range(2):
+                        half = slice(parity * PAIRS * P, (parity + 1) * PAIRS * P)
+                        nc.vector.quantize_mx(out=t_codes[:, g, half].bitcast(FP8X4), scales=t_scales[:, g, half],
+                                              in_=grouped[parity][:])
+                        if parity == 0:
+                            multiply(g, 0)
+                            if last:
+                                for earlier in range(PASSES - 1):
+                                    multiply(earlier, 1)
+                        elif last:
+                            multiply(g, 1)
+                    if g + 2 < PASSES:
+                        widen(g + 2)
+
+            for q in range(PAIRS):
+                if q % 2 == 0:
+                    nc.scalar.copy(out=f_sb[:, 2 * q:2 * q + 2, :], in_=f_bank[q][:])
+                else:
+                    nc.vector.tensor_copy(out=f_sb[:, 2 * q:2 * q + 2, :], in_=f_bank[q][:])
+
+        s_sum = keep.tile([P, ROWS], F32, name="s_sum")
+        nc.vector.tensor_reduce(out=s_sum[:], in_=f_sb[:].rearrange("p k n -> p n k"), axis=AX.X, op=ALU.add)
+        minus_half_s = keep.tile([P, ROWS], F32, name="minus_half_s")
+        nc.vector.tensor_scalar(out=minus_half_s[:], in0=s_sum[:], scalar1=-0.5, scalar2=None, op0=ALU.mult)
+
+        f_t = keep.tile([P, 2, KK, P], F32, name="f_t")
+        acc_pool = ctx.enter_context(tc.tile_pool(name="acc_pool", bufs=2))
+        exp_pool = ctx.enter_context(tc.tile_pool(name="exp_pool", bufs=9))
+        term_pool = ctx.enter_context(tc.tile_pool(name="term_pool", bufs=2))
+        turned_pool = ctx.enter_context(tc.tile_pool(name="turned_pool", bufs=2))
+
+        vector_groups = list(range(GPSIMD_ROWS, SPLIT, GROUP))
+        per_batch = BATCH // GROUP
+        batches = [vector_groups[i:i + per_batch] for i in range(0, len(vector_groups), per_batch)]
+        visits = [(b, q) for b in range(len(batches)) for q in range(PAIRS)]
+        scalar_chunks = cut_into_chunks(list(range(SPLIT, ROWS, GROUP)))
+        gpsimd_chunks = cut_into_chunks(list(range(0, GPSIMD_ROWS, GROUP)))
+
+        ring = {}
+        for v in range(RING):
+            ring[v] = f_bank[v]
+        acc_of = {}
+        jobs = []
+        exp_of = {}
+        cols_due = []
+
+        def transpose_f(q):
+            landing = psum.tile([P, 2, 2, P], F32, name="f_t_bank", tag="bank%d" % (RING + q % 4))
+            for s in range(2):
+                for h in range(2):
+                    nc.tensor.transpose(landing[:, s, h, :], f_sb[:, 2 * q + s, h * P:(h + 1) * P], ident[:])
+            dst = f_t[:, :, 2 * q:2 * q + 2, :].rearrange("p h k j -> p k h j")
+            if q % 2 == 0:
+                nc.scalar.copy(out=dst, in_=landing[:])
+            else:
+                nc.vector.tensor_copy(out=dst, in_=landing[:])
+
+        def refill(v):
+            q = visits[v][1]
+            bank = psum.tile([P, 2, ROWS], F32, name="ring", tag="bank%d" % (v % RING))
+            for s in range(2):
+                for h in range(2):
+                    nc.tensor.transpose(bank[:, s, h * P:(h + 1) * P], f_t[:, h, 2 * q + s, :], ident[:])
+            ring[v] = bank
+
+        def vector_visit(v):
+            b, q = visits[v]
+            if q == 0:
+                acc_new = acc_pool.tile([P, BATCH, ROWS - GPSIMD_ROWS], F32, name="acc", tag="acc")
+                acc_of[b] = acc_new
+            acc = acc_of[b]
+            for s in range(2):
+                k = 2 * q + s
+                for gi, m0 in enumerate(batches[b]):
+                    width = ROWS - m0
+                    for r in range(GROUP):
+                        row = gi * GROUP + r
+                        m = m0 + r
+                        nc.vector.scalar_tensor_tensor(
+                            out=acc[:, row, 0:width],
+                            in0=ring[v][:, s, m0:ROWS],
+                            scalar=f_sb[:, k, m:m + 1],
+                            in1=(minus_half_s[:, m0:ROWS] if k == 0 else acc[:, row, 0:width]),
+                            op0=ALU.max,
+                            op1=ALU.add,
+                        )
+
+        def vector_exp(b, step):
+            for gi, m0 in enumerate(batches[b]):
+                width = ROWS - m0
+                e = exp_pool.tile([P, GROUP, width], F32, name="e", tag="e")
+                for r in range(GROUP):
+                    m = m0 + r
+                    nc.scalar.activation(out=e[:, r, :], in_=acc_of[b][:, gi * GROUP + r, 0:width], func=ACT.Exp,
+                                         bias=s_sum[:, m:m + 1], scale=-2.0, accum_out=row_sums[:, m:m + 1])
+                cols_due.append((e, m0, step))
+
+        def scalar_terms(chunk):
+            terms = term_pool.tile([P, KK, CHUNK], F32, name="abs_terms", tag="abs_terms")
+            for m0, r, c0, c1, place in filled_up(chunk):
+                m = m0 + r
+                for k in range(KK):
+                    nc.scalar.activation(out=terms[:, k, place:place + c1 - c0], in_=f_sb[:, k, m0 + c0:m0 + c1], func=ACT.Abs,
+                                         bias=f_sb[:, k, m:m + 1], scale=-1.0)
+            return (terms, KK, chunk, False)
+
+        def gpsimd_terms(chunk):
+            terms = term_pool.tile([P, KK + 1, CHUNK], F32, name="max_terms", tag="max_terms")
+            for m0, r, c0, c1, place in filled_up(chunk):
+                m = m0 + r
+                for k in range(KK):
+                    nc.gpsimd.tensor_scalar(out=terms[:, k, place:place + c1 - c0], in0=f_sb[:, k, m0 + c0:m0 + c1], scalar1=BIG,
+                                            scalar2=f_sb[:, k, m:m + 1], op0=ALU.min, op1=ALU.max)
+                nc.gpsimd.tensor_scalar(out=terms[:, KK, place:place + c1 - c0], in0=minus_half_s[:, m0 + c0:m0 + c1], scalar1=1.0,
+                                        scalar2=0.0, op0=ALU.mult, op1=ALU.add)
+            return (terms, KK + 1, chunk, True)
+
+        def add_terms(made):
+            terms, count, chunk, is_max = made
+            summed = psum.tile([P, CHUNK // P, P], F32, name="summed", tag="bank%d" % (RING + len(jobs) % 2))
+            for t in range(tiles_of(chunk)):
+                for i in range(count):
+                    nc.tensor.matmul(out=summed[:, t, :], lhsT=terms[:, i, t * P:(t + 1) * P], rhs=ident[:], start=(i == 0),
+                                     stop=(i == count - 1), is_transpose=True)
+            jobs.append([chunk, is_max, summed])
+
+        def turn_back(number):
+            chunk, is_max, summed = jobs[number]
+            tiles = tiles_of(chunk)
+            turned = turned_pool.tile([P, CHUNK // P, P], F32, name="turned", tag="turned")
+            nc.scalar.copy(out=turned[:, 0:tiles, :], in_=summed[:, 0:tiles, :])
+            sums = psum.tile([P, CHUNK], F32, name="sums", tag="bank%d" % (RING + 2 + number % 2))
+            for t in range(tiles):
+                nc.tensor.transpose(sums[:, t * P:(t + 1) * P], turned[:, t, :], ident[:])
+            jobs[number].append(sums)
+
+        def chunk_exp(number, step):
+            chunk, is_max, summed, sums = jobs[number]
+            for m0, r, c0, c1, place in chunk:
+                width = ROWS - m0
+                m = m0 + r
+                if m0 not in exp_of:
+                    e_new = exp_pool.tile([P, GROUP, width], F32, name="e", tag="e")
+                    exp_of[m0] = e_new
+                total = row_sums if c0 == 0 else row_sums2
+                if is_max:
+                    nc.scalar.activation(out=exp_of[m0][:, r, c0:c1], in_=sums[:, place:place + c1 - c0], func=ACT.Exp,
+                                         bias=s_sum[:, m:m + 1], scale=-2.0, accum_out=total[:, m:m + 1])
+                else:
+                    nc.scalar.activation(out=exp_of[m0][:, r, c0:c1], in_=sums[:, place:place + c1 - c0], func=ACT.Exp,
+                                         scale=-1.0, accum_out=total[:, m:m + 1])
+                if r == GROUP - 1 and c1 == width:
+                    cols_due.append((exp_of[m0], m0, step))
+
+        def add_columns(before):
+            while cols_due and cols_due[0][2] < before:
+                e, m0, issued = cols_due.pop(0)
+                beyond = m0 + GROUP
+                if beyond < ROWS:
+                    nc.gpsimd.tensor_tensor(out=col_sums[:, :, beyond:ROWS], in0=col_sums[:, :, beyond:ROWS], in1=e[:, :, GROUP:],
+                                            op=ALU.add)
+
+        def chunk_step(made, step):
+            if made:
+                add_terms(made)
+            else:
+                jobs.append(None)
+            newest = len(jobs) - 1
+            if newest >= 1 and jobs[newest - 1]:
+                turn_back(newest - 1)
+            if newest >= 2 and jobs[newest - 2]:
+                chunk_exp(newest - 2, step)
+
+        visit_work = [float(sum([ROWS - m0 for m0 in batches[b]])) for b, q in visits]
+        vector_total = sum(visit_work)
+        vector_done = 0.0
+        v = 0
+        i_s = 0
+        i_g = 0
+        step = 0
+        waiting = []
+
+        with tc.manual_schedule():
+            for q in (4, 5, 6, 7, 0, 1, 2, 3):
+                transpose_f(q)
+            while v < len(visits) or i_s < len(scalar_chunks) or i_g < len(gpsimd_chunks):
+                shares = []
+                if v < len(visits):
+                    shares.append((vector_done / vector_total, 0))
+                if i_s < len(scalar_chunks):
+                    shares.append((i_s / float(len(scalar_chunks)), 1))
+                if i_g < len(gpsimd_chunks):
+                    shares.append((i_g / float(len(gpsimd_chunks)), 2))
+                route = min(shares)[1]
+                step += 1
+                if route == 0:
+                    vector_visit(v)
+                    if RING <= v + 2 < len(visits):
+                        refill(v + 2)
+                    add_columns(step - 1)
+                    if visits[v][1] == EXP_LAG and visits[v][0] > 0:
+                        vector_exp(visits[v][0] - 1, step)
+                    vector_done += visit_work[v]
+                    v += 1
+                elif route == 1:
+                    chunk_step(scalar_terms(scalar_chunks[i_s]), step)
+                    add_columns(step - 1)
+                    i_s += 1
+                else:
+                    for made in waiting:
+                        chunk_step(made, step)
+                    waiting = [gpsimd_terms(gpsimd_chunks[i_g])]
+                    add_columns(step - 1)
+                    i_g += 1
+            for made in waiting:
+                step += 1
+                chunk_step(made, step)
+            vector_exp(len(batches) - 1, step)
+            for i in range(2):
+                step += 1
+                chunk_step(None, step)
+            add_columns(step + 1)
+
+        diversity = psum.tile([P, 2, P], F32, name="diversity", tag="bank0")
+        for h in range(2):
+            block = slice(h * P, (h + 1) * P)
+            for r in range(GROUP):
+                nc.tensor.matmul(out=diversity[:, h, :], lhsT=col_sums[:, r, block], rhs=ident[:], start=(r == 0), stop=False,
+                                 is_transpose=True)
+            nc.tensor.matmul(out=diversity[:, h, :], lhsT=row_sums2[:, block], rhs=ident[:], start=False, stop=False,
+                             is_transpose=True)
+            nc.tensor.matmul(out=diversity[:, h, :], lhsT=row_sums[:, block], rhs=ident[:], start=False, stop=True,
+                             is_transpose=True)
+        diversity_sb = keep.tile([P, 2, P], F32, name="diversity_sb")
+        nc.vector.tensor_copy(out=diversity_sb[:], in_=diversity[:])
+        nc.sync.dma_start(out=out[:, IN_F:IN_F + P].rearrange("(h p) j -> p h j", p=P), in_=diversity_sb[:])

@@ -17,56 +17,31 @@ AX = mybir.AxisListType
 
 P = 128
 ROWS = 256
+EXT = ROWS + P
 IN_F = 2048
 PACK = 4
 PASSES = IN_F // (P * PACK)
 KK = 16
 PAIRS = KK // 2
 RING = 4
+JOB_BANKS = 3
 GROUP = 4
 BATCH = 16
-CHUNK = 384
-GPSIMD_ROWS = 20
-SPLIT = 116
+VECTOR_ROWS = 124
+SCALAR_ROWS = 92
+SCALAR_JOB = 4
+GPSIMD_JOB = 2
 EXP_LAG = 2
 BIG = 3.0e38
+PLANE = ROWS
+HALF = IN_F // 2
+VECTOR_COLS = 384
 
 
-def cut_into_chunks(first_rows):
-    chunks = []
-    segments = []
-    used = 0
-    for m0 in first_rows:
-        width = ROWS - m0
-        for r in range(GROUP):
-            c = 0
-            while c < width:
-                take = min(width - c, CHUNK - used)
-                segments.append((m0, r, c, c + take, used))
-                used += take
-                c += take
-                if used == CHUNK:
-                    chunks.append(segments)
-                    segments = []
-                    used = 0
-    if used:
-        chunks.append(segments)
-    return chunks
-
-
-def columns_used(chunk):
-    return chunk[-1][4] + chunk[-1][3] - chunk[-1][2]
-
-
-def tiles_of(chunk):
-    return (columns_used(chunk) + P - 1) // P
-
-
-def filled_up(chunk):
-    spare = tiles_of(chunk) * P - columns_used(chunk)
-    if spare:
-        return chunk + [(0, 0, 0, spare, columns_used(chunk))]
-    return chunk
+def first_column(m):
+    if m < P:
+        return m + 1
+    return m
 
 
 def tile_minibatchdiscriminator_kernel(tc, tensor, T_bytes, T_scale, out):
@@ -81,13 +56,24 @@ def tile_minibatchdiscriminator_kernel(tc, tensor, T_bytes, T_scale, out):
 
         ident = keep.tile([P, P], F32, name="ident")
         make_identity(nc, ident[:])
-        col_sums = keep.tile([P, GROUP, ROWS], F32, name="col_sums")
+        zeros = keep.tile([P, P], F32, name="zeros")
+        nc.gpsimd.memset(zeros[:], 0.0)
+        ones = keep.tile([P, 1], F32, name="ones")
+        nc.gpsimd.memset(ones[:], 1.0)
+        not_first = keep.tile([P, 1], F32, name="not_first")
+        nc.vector.tensor_scalar(out=not_first[:], in0=ident[:, 0:1], scalar1=-1.0, scalar2=1.0, op0=ALU.mult, op1=ALU.add)
+        col_sums = keep.tile([P, GROUP * (PLANE + 1) + P], F32, name="col_sums")
         nc.gpsimd.memset(col_sums[:], 0.0)
+        nc.gpsimd.memset(col_sums[:, 0:P], 1.0)
         row_sums = keep.tile([P, ROWS], F32, name="row_sums")
-        row_sums2 = keep.tile([P, ROWS], F32, name="row_sums2")
-        nc.gpsimd.memset(row_sums2[:], 0.0)
+        totals_sb = keep.tile([P, EXT], F32, name="totals_sb")
+        nc.gpsimd.memset(totals_sb[:], 0.0)
 
-        f_sb = keep.tile([P, KK, ROWS], F32, name="f_sb")
+        f_ext = keep.tile([P, KK, EXT], F32, name="f_ext")
+        f_t = keep.tile([P, 2, KK, P], F32, name="f_t")
+        s_t = keep.tile([P, 2, P], F32, name="s_t")
+        s_sum = keep.tile([P, ROWS], F32, name="s_sum")
+        minus_half_s = keep.tile([P, EXT], F32, name="minus_half_s")
         f_bank = []
 
         with ExitStack() as head:
@@ -95,11 +81,10 @@ def tile_minibatchdiscriminator_kernel(tc, tensor, T_bytes, T_scale, out):
             stage = head.enter_context(tc.tile_pool(name="stage", bufs=2))
             mxp = head.enter_context(tc.tile_pool(name="mxp", bufs=1))
 
-            x_sb = mxp.tile([P, 2, IN_F], BF16, name="x_sb")
-            nc.sync.dma_start(out=x_sb[:], in_=tensor.rearrange("(h p) i -> p h i", p=P))
             t_scale = mxp.tile([P, PASSES, PACK], F32, name="t_scale")
             nc.scalar.dma_start(out=t_scale[:], in_=T_scale.rearrange("(g p t) a b -> p g (t a b)", p=P, t=PACK))
             bytes_view = T_bytes.rearrange("(g p t) j k -> g p (t j k)", p=P, t=PACK)
+            x_sb = mxp.tile([P, 2, IN_F], BF16, name="x_sb")
             t_bytes = []
             for g in range(PASSES):
                 tb = bytes_pool.tile([P, PACK * IN_F], U8, name="t_bytes%d" % g)
@@ -107,6 +92,8 @@ def tile_minibatchdiscriminator_kernel(tc, tensor, T_bytes, T_scale, out):
                     run = slice(piece * 4096, (piece + 1) * 4096)
                     nc.sync.dma_start(out=tb[:, run], in_=bytes_view[g][:, run])
                 t_bytes.append(tb)
+                if g == 0:
+                    nc.sync.dma_start(out=x_sb[:], in_=tensor.rearrange("(h p) i -> p h i", p=P))
 
             x_f32 = mxp.tile([P, 2, IN_F], F32, name="x_f32")
             out_x = out[:, 0:IN_F].rearrange("(h p) i -> p h i", p=P)
@@ -116,6 +103,8 @@ def tile_minibatchdiscriminator_kernel(tc, tensor, T_bytes, T_scale, out):
             t_codes = mxp.tile([P, PASSES, IN_F], U32, name="t_codes", align_bytes=64)
             t_scales = mxp.tile([P, PASSES, IN_F], U8, name="t_scales", align_bytes=64)
             widened = {}
+            grouped_of = {}
+            ft_bank = {}
 
             def widen(g):
                 w = stage.tile([P, PACK, IN_F], BF16, name="w", tag="w")
@@ -124,29 +113,36 @@ def tile_minibatchdiscriminator_kernel(tc, tensor, T_bytes, T_scale, out):
                     nc.vector.tensor_scalar(out=w[:, t, :], in0=t_bytes[g][:, t * IN_F:(t + 1) * IN_F].bitcast(FP8),
                                             scalar1=t_scale[:, g, t:t + 1], scalar2=None, op0=ALU.mult)
 
-            def interleave(g, parity, grouped, j0, j1, on_scalar):
-                dst = grouped[:].rearrange("p (c j t) -> p c j t", c=PAIRS, t=PACK)[:, :, j0:j1, :]
-                src = widened[g][:].rearrange("p t (j k) -> p k j t", k=KK)[:, parity:KK:2, j0:j1, :]
+            def interleave(g, half, c0, c1, on_scalar):
+                dst = grouped_of[(g, half)][:].rearrange("p (c t) -> p c t", t=PACK)[:, c0:c1, :]
+                src = widened[g][:, :, half * HALF + c0:half * HALF + c1].rearrange("p t c -> p c t")
                 if on_scalar:
                     nc.scalar.copy(out=dst, in_=src)
                 else:
                     nc.vector.tensor_copy(out=dst, in_=src)
 
-            def multiply(g, parity):
-                for q in range(PAIRS):
-                    cols = slice((PAIRS * parity + q) * P, (PAIRS * parity + q + 1) * P)
-                    x_cols = slice(g * ROWS, (g + 1) * ROWS)
-                    nc.tensor.matmul_mx(
-                        out=f_bank[q][:, parity, :],
-                        lhsT=t_codes[:, g, cols].bitcast(FP8X4),
-                        lhsT_scale=t_scales[:, g, cols],
-                        rhs=x_codes[:, x_cols].bitcast(FP8X4),
-                        rhs_scale=x_scales[:, x_cols],
-                        start=(g == 0),
-                        stop=(g == PASSES - 1),
-                    )
+            def quantize(g, half):
+                cols = slice(half * HALF, (half + 1) * HALF)
+                nc.vector.quantize_mx(out=t_codes[:, g, cols].bitcast(FP8X4), scales=t_scales[:, g, cols],
+                                      in_=grouped_of[(g, half)][:])
+
+            def multiply(g, half):
+                for cb in (2 * half, 2 * half + 1):
+                    for h in range(2):
+                        cols = slice(cb * 512, (cb + 1) * 512)
+                        x_cols = slice(g * ROWS + h * P, g * ROWS + (h + 1) * P)
+                        nc.tensor.matmul_mx(
+                            out=ft_bank[(h, cb)][:],
+                            lhsT=x_codes[:, x_cols].bitcast(FP8X4),
+                            lhsT_scale=x_scales[:, x_cols],
+                            rhs=t_codes[:, g, cols].bitcast(FP8X4),
+                            rhs_scale=t_scales[:, g, cols],
+                            start=(g == 0),
+                            stop=(g == PASSES - 1),
+                        )
 
             with tc.manual_schedule():
+                widen(0)
                 for g in range(PASSES):
                     x_t = psum.tile([P, 2, 2, P], F32, name="x_t%d" % g, tag="bank%d" % g)
                     for h in range(2):
@@ -158,84 +154,87 @@ def tile_minibatchdiscriminator_kernel(tc, tensor, T_bytes, T_scale, out):
                         in_=x_t[:].rearrange("p h u r -> p h r u"),
                     )
                 for h in range(2):
-                    nc.scalar.copy(out=x_f32[:, h, :], in_=x_sb[:, h, :])
+                    for cb in range(4):
+                        bank = psum.tile([P, 512], F32, name="ft_bank%d" % (4 * h + cb), tag="bank%d" % (4 * h + cb))
+                        ft_bank[(h, cb)] = bank
+                for g in range(PASSES):
+                    last = g == PASSES - 1
+                    for half in range(2):
+                        t_grouped = stage.tile([P, HALF * PACK], BF16, name="t_grouped", tag="t_grouped", bufs=4, align_bytes=64)
+                        grouped_of[(g, half)] = t_grouped
+                    interleave(g, 0, 0, HALF, True)
+                    if last:
+                        interleave(g, 1, 0, HALF, False)
+                    else:
+                        interleave(g, 1, VECTOR_COLS, HALF, True)
+                        interleave(g, 1, 0, VECTOR_COLS, False)
+                    if g == 0:
+                        nc.vector.quantize_mx(out=x_codes[:].bitcast(FP8X4), scales=x_scales[:],
+                                              in_=x_grouped[:].rearrange("p g c -> p (g c)"))
+                    else:
+                        for half in range(2):
+                            quantize(g - 1, half)
+                            multiply(g - 1, half)
+                    if not last:
+                        widen(g + 1)
+                for half in (1, 0):
+                    quantize(PASSES - 1, half)
+                    multiply(PASSES - 1, half)
+                for h in range(2):
+                    nc.vector.tensor_copy(out=x_f32[:, h, :], in_=x_sb[:, h, :])
                     nc.sync.dma_start(out=out_x[:, h, :], in_=x_f32[:, h, :])
-                widen(0)
-                nc.vector.quantize_mx(out=x_codes[:].bitcast(FP8X4), scales=x_scales[:],
-                                      in_=x_grouped[:].rearrange("p g c -> p (g c)"))
-                widen(1)
+
+                closing = [(h, cb) for cb in (2, 3, 0, 1) for h in range(2)]
+                for i, (h, cb) in enumerate(closing):
+                    dst = f_t[:, h, :, cb * 32:(cb + 1) * 32]
+                    src = ft_bank[(h, cb)][:].rearrange("p (j k) -> p k j", k=KK)
+                    if i < len(closing) - 2:
+                        nc.scalar.copy(out=dst, in_=src)
+                    else:
+                        nc.vector.tensor_copy(out=dst, in_=src)
+                for h, cb in closing:
+                    nc.vector.tensor_reduce(out=s_t[:, h, cb * 32:(cb + 1) * 32],
+                                            in_=f_t[:, h, :, cb * 32:(cb + 1) * 32].rearrange("p k j -> p j k"), axis=AX.X, op=ALU.add)
                 for q in range(PAIRS):
                     bank = psum.tile([P, 2, ROWS], F32, name="f_bank%d" % q, tag="bank%d" % q)
                     f_bank.append(bank)
-                for g in range(PASSES):
-                    last = g == PASSES - 1
-                    grouped = []
-                    for parity in range(2):
-                        t_grouped = stage.tile([P, PAIRS * P * PACK], BF16, name="t_grouped", tag="t_grouped", bufs=4,
-                                               align_bytes=64)
-                        grouped.append(t_grouped)
-                    if last:
-                        interleave(g, 0, grouped[0], P // 2, P, True)
-                        interleave(g, 0, grouped[0], 0, P // 2, False)
-                    else:
-                        interleave(g, 0, grouped[0], 0, P, False)
-                    interleave(g, 1, grouped[1], 0, P, True)
-                    for parity in range(2):
-                        half = slice(parity * PAIRS * P, (parity + 1) * PAIRS * P)
-                        nc.vector.quantize_mx(out=t_codes[:, g, half].bitcast(FP8X4), scales=t_scales[:, g, half],
-                                              in_=grouped[parity][:])
-                        if parity == 0:
-                            multiply(g, 0)
-                            if last:
-                                for earlier in range(PASSES - 1):
-                                    multiply(earlier, 1)
-                        elif last:
-                            multiply(g, 1)
-                    if g + 2 < PASSES:
-                        widen(g + 2)
+                    for s in range(2):
+                        for h in range(2):
+                            nc.tensor.transpose(bank[:, s, h * P:(h + 1) * P], f_t[:, h, 2 * q + s, :], ident[:])
+                    nc.scalar.copy(out=f_ext[:, 2 * q:2 * q + 2, 0:ROWS], in_=bank[:])
+                s_bank = psum.tile([P, ROWS], F32, name="s_bank", tag="bank7")
+                for h in range(2):
+                    nc.tensor.transpose(s_bank[:, h * P:(h + 1) * P], s_t[:, h, :], ident[:])
+                nc.vector.tensor_copy(out=s_sum[:], in_=s_bank[:])
+                nc.vector.tensor_scalar(out=minus_half_s[:, 0:ROWS], in0=s_sum[:], scalar1=-0.5, scalar2=None, op0=ALU.mult)
+                nc.vector.tensor_scalar(out=minus_half_s[:, ROWS:EXT], in0=s_sum[:, 0:P], scalar1=-0.5, scalar2=None, op0=ALU.mult)
 
-            for q in range(PAIRS):
-                if q % 2 == 0:
-                    nc.scalar.copy(out=f_sb[:, 2 * q:2 * q + 2, :], in_=f_bank[q][:])
-                else:
-                    nc.vector.tensor_copy(out=f_sb[:, 2 * q:2 * q + 2, :], in_=f_bank[q][:])
+        nc.gpsimd.tensor_scalar(out=f_ext[:, :, ROWS:EXT], in0=f_ext[:, :, 0:P], scalar1=1.0, scalar2=0.0, op0=ALU.mult,
+                                op1=ALU.add)
 
-        s_sum = keep.tile([P, ROWS], F32, name="s_sum")
-        nc.vector.tensor_reduce(out=s_sum[:], in_=f_sb[:].rearrange("p k n -> p n k"), axis=AX.X, op=ALU.add)
-        minus_half_s = keep.tile([P, ROWS], F32, name="minus_half_s")
-        nc.vector.tensor_scalar(out=minus_half_s[:], in0=s_sum[:], scalar1=-0.5, scalar2=None, op0=ALU.mult)
-
-        f_t = keep.tile([P, 2, KK, P], F32, name="f_t")
         acc_pool = ctx.enter_context(tc.tile_pool(name="acc_pool", bufs=2))
         exp_pool = ctx.enter_context(tc.tile_pool(name="exp_pool", bufs=9))
-        term_pool = ctx.enter_context(tc.tile_pool(name="term_pool", bufs=2))
-        turned_pool = ctx.enter_context(tc.tile_pool(name="turned_pool", bufs=2))
+        term_pool = ctx.enter_context(tc.tile_pool(name="term_pool", bufs=4))
+        turned_pool = ctx.enter_context(tc.tile_pool(name="turned_pool", bufs=3))
 
-        vector_groups = list(range(GPSIMD_ROWS, SPLIT, GROUP))
+        vector_groups = list(range(0, VECTOR_ROWS, GROUP))
         per_batch = BATCH // GROUP
         batches = [vector_groups[i:i + per_batch] for i in range(0, len(vector_groups), per_batch)]
         visits = [(b, q) for b in range(len(batches)) for q in range(PAIRS)]
-        scalar_chunks = cut_into_chunks(list(range(SPLIT, ROWS, GROUP)))
-        gpsimd_chunks = cut_into_chunks(list(range(0, GPSIMD_ROWS, GROUP)))
+        scalar_rows = list(range(VECTOR_ROWS, VECTOR_ROWS + SCALAR_ROWS))
+        gpsimd_rows = list(range(VECTOR_ROWS + SCALAR_ROWS, ROWS))
+        row_slot = EXT - VECTOR_ROWS
+        rows_left = [ROWS - VECTOR_ROWS]
 
         ring = {}
         for v in range(RING):
             ring[v] = f_bank[v]
         acc_of = {}
-        jobs = []
-        exp_of = {}
         cols_due = []
-
-        def transpose_f(q):
-            landing = psum.tile([P, 2, 2, P], F32, name="f_t_bank", tag="bank%d" % (RING + q % 4))
-            for s in range(2):
-                for h in range(2):
-                    nc.tensor.transpose(landing[:, s, h, :], f_sb[:, 2 * q + s, h * P:(h + 1) * P], ident[:])
-            dst = f_t[:, :, 2 * q:2 * q + 2, :].rearrange("p h k j -> p k h j")
-            if q % 2 == 0:
-                nc.scalar.copy(out=dst, in_=landing[:])
-            else:
-                nc.vector.tensor_copy(out=dst, in_=landing[:])
+        jobs = []
+        open_job = []
+        ready = []
+        waiting = []
 
         def refill(v):
             q = visits[v][1]
@@ -248,131 +247,114 @@ def tile_minibatchdiscriminator_kernel(tc, tensor, T_bytes, T_scale, out):
         def vector_visit(v):
             b, q = visits[v]
             if q == 0:
-                acc_new = acc_pool.tile([P, BATCH, ROWS - GPSIMD_ROWS], F32, name="acc", tag="acc")
+                acc_new = acc_pool.tile([P, BATCH, P], F32, name="acc", tag="acc")
                 acc_of[b] = acc_new
             acc = acc_of[b]
             for s in range(2):
                 k = 2 * q + s
                 for gi, m0 in enumerate(batches[b]):
-                    width = ROWS - m0
                     for r in range(GROUP):
                         row = gi * GROUP + r
                         m = m0 + r
+                        c = first_column(m)
                         nc.vector.scalar_tensor_tensor(
-                            out=acc[:, row, 0:width],
-                            in0=ring[v][:, s, m0:ROWS],
-                            scalar=f_sb[:, k, m:m + 1],
-                            in1=(minus_half_s[:, m0:ROWS] if k == 0 else acc[:, row, 0:width]),
+                            out=acc[:, row, :],
+                            in0=ring[v][:, s, c:c + P],
+                            scalar=f_ext[:, k, m:m + 1],
+                            in1=(minus_half_s[:, c:c + P] if k == 0 else acc[:, row, :]),
                             op0=ALU.max,
                             op1=ALU.add,
                         )
 
         def vector_exp(b, step):
             for gi, m0 in enumerate(batches[b]):
-                width = ROWS - m0
-                e = exp_pool.tile([P, GROUP, width], F32, name="e", tag="e")
+                e = exp_pool.tile([P, GROUP, P], F32, name="e", tag="e")
                 for r in range(GROUP):
                     m = m0 + r
-                    nc.scalar.activation(out=e[:, r, :], in_=acc_of[b][:, gi * GROUP + r, 0:width], func=ACT.Exp,
+                    nc.scalar.activation(out=e[:, r, :], in_=acc_of[b][:, gi * GROUP + r, :], func=ACT.Exp,
                                          bias=s_sum[:, m:m + 1], scale=-2.0, accum_out=row_sums[:, m:m + 1])
                 cols_due.append((e, m0, step))
-
-        def scalar_terms(chunk):
-            terms = term_pool.tile([P, KK, CHUNK], F32, name="abs_terms", tag="abs_terms")
-            for m0, r, c0, c1, place in filled_up(chunk):
-                m = m0 + r
-                for k in range(KK):
-                    nc.scalar.activation(out=terms[:, k, place:place + c1 - c0], in_=f_sb[:, k, m0 + c0:m0 + c1], func=ACT.Abs,
-                                         bias=f_sb[:, k, m:m + 1], scale=-1.0)
-            return (terms, KK, chunk, False)
-
-        def gpsimd_terms(chunk):
-            terms = term_pool.tile([P, KK + 1, CHUNK], F32, name="max_terms", tag="max_terms")
-            for m0, r, c0, c1, place in filled_up(chunk):
-                m = m0 + r
-                for k in range(KK):
-                    nc.gpsimd.tensor_scalar(out=terms[:, k, place:place + c1 - c0], in0=f_sb[:, k, m0 + c0:m0 + c1], scalar1=BIG,
-                                            scalar2=f_sb[:, k, m:m + 1], op0=ALU.min, op1=ALU.max)
-                nc.gpsimd.tensor_scalar(out=terms[:, KK, place:place + c1 - c0], in0=minus_half_s[:, m0 + c0:m0 + c1], scalar1=1.0,
-                                        scalar2=0.0, op0=ALU.mult, op1=ALU.add)
-            return (terms, KK + 1, chunk, True)
-
-        def add_terms(made):
-            terms, count, chunk, is_max = made
-            summed = psum.tile([P, CHUNK // P, P], F32, name="summed", tag="bank%d" % (RING + len(jobs) % 2))
-            for t in range(tiles_of(chunk)):
-                for i in range(count):
-                    nc.tensor.matmul(out=summed[:, t, :], lhsT=terms[:, i, t * P:(t + 1) * P], rhs=ident[:], start=(i == 0),
-                                     stop=(i == count - 1), is_transpose=True)
-            jobs.append([chunk, is_max, summed])
-
-        def turn_back(number):
-            chunk, is_max, summed = jobs[number]
-            tiles = tiles_of(chunk)
-            turned = turned_pool.tile([P, CHUNK // P, P], F32, name="turned", tag="turned")
-            nc.scalar.copy(out=turned[:, 0:tiles, :], in_=summed[:, 0:tiles, :])
-            sums = psum.tile([P, CHUNK], F32, name="sums", tag="bank%d" % (RING + 2 + number % 2))
-            for t in range(tiles):
-                nc.tensor.transpose(sums[:, t * P:(t + 1) * P], turned[:, t, :], ident[:])
-            jobs[number].append(sums)
-
-        def chunk_exp(number, step):
-            chunk, is_max, summed, sums = jobs[number]
-            for m0, r, c0, c1, place in chunk:
-                width = ROWS - m0
-                m = m0 + r
-                if m0 not in exp_of:
-                    e_new = exp_pool.tile([P, GROUP, width], F32, name="e", tag="e")
-                    exp_of[m0] = e_new
-                total = row_sums if c0 == 0 else row_sums2
-                if is_max:
-                    nc.scalar.activation(out=exp_of[m0][:, r, c0:c1], in_=sums[:, place:place + c1 - c0], func=ACT.Exp,
-                                         bias=s_sum[:, m:m + 1], scale=-2.0, accum_out=total[:, m:m + 1])
-                else:
-                    nc.scalar.activation(out=exp_of[m0][:, r, c0:c1], in_=sums[:, place:place + c1 - c0], func=ACT.Exp,
-                                         scale=-1.0, accum_out=total[:, m:m + 1])
-                if r == GROUP - 1 and c1 == width:
-                    cols_due.append((exp_of[m0], m0, step))
 
         def add_columns(before):
             while cols_due and cols_due[0][2] < before:
                 e, m0, issued = cols_due.pop(0)
-                beyond = m0 + GROUP
-                if beyond < ROWS:
-                    nc.gpsimd.tensor_tensor(out=col_sums[:, :, beyond:ROWS], in0=col_sums[:, :, beyond:ROWS], in1=e[:, :, GROUP:],
-                                            op=ALU.add)
+                slanted = col_sums[:, m0 + 1:m0 + 1 + GROUP * (PLANE + 1)].rearrange("p (r w) -> p r w", w=PLANE + 1)[:, :, 0:P]
+                nc.gpsimd.tensor_tensor(out=slanted, in0=slanted, in1=e[:], op=ALU.add)
 
-        def chunk_step(made, step):
-            if made:
-                add_terms(made)
-            else:
-                jobs.append(None)
-            newest = len(jobs) - 1
-            if newest >= 1 and jobs[newest - 1]:
-                turn_back(newest - 1)
-            if newest >= 2 and jobs[newest - 2]:
-                chunk_exp(newest - 2, step)
+        def scalar_terms(m):
+            terms = term_pool.tile([P, KK, P], F32, name="abs_terms", tag="abs_terms")
+            c = first_column(m)
+            for k in range(KK):
+                nc.scalar.activation(out=terms[:, k, :], in_=f_ext[:, k, c:c + P], func=ACT.Abs, bias=f_ext[:, k, m:m + 1],
+                                     scale=-1.0)
+            return [terms[:, k, :] for k in range(KK)]
 
-        visit_work = [float(sum([ROWS - m0 for m0 in batches[b]])) for b, q in visits]
-        vector_total = sum(visit_work)
-        vector_done = 0.0
+        def gpsimd_terms(m):
+            terms = term_pool.tile([P, KK, P], F32, name="max_terms", tag="max_terms")
+            c = first_column(m)
+            for k in range(KK):
+                nc.gpsimd.tensor_scalar(out=terms[:, k, :], in0=f_ext[:, k, c:c + P], scalar1=BIG, scalar2=f_ext[:, k, m:m + 1],
+                                        op0=ALU.min, op1=ALU.max)
+            s_term = term_pool.tile([P, P], F32, name="s_term", tag="s_term")
+            nc.vector.tensor_scalar(out=s_term[:], in0=minus_half_s[:, c:c + P], scalar1=minus_half_s[:, m:m + 1], scalar2=None,
+                                    op0=ALU.add)
+            return [terms[:, k, :] for k in range(KK)] + [s_term[:]]
+
+        def new_job(size, scale):
+            bank = psum.tile([P, size, P], F32, name="job", tag="bank%d" % (RING + len(jobs) % JOB_BANKS))
+            job = [[], bank, scale]
+            jobs.append(job)
+            return job
+
+        def add_terms(job, m, pieces):
+            slot = len(job[0])
+            job[0].append(m)
+            for i, piece in enumerate(pieces):
+                nc.tensor.matmul(out=job[1][:, slot, :], lhsT=piece, rhs=ident[:], start=(i == 0), stop=(i == len(pieces) - 1),
+                                 is_transpose=True)
+
+        def finish(job):
+            rows, bank, scale = job
+            turned = turned_pool.tile([P, SCALAR_JOB, P], F32, name="turned", tag="turned")
+            nc.scalar.activation(out=turned[:, 0:len(rows), :], in_=bank[:, 0:len(rows), :], func=ACT.Exp, scale=scale)
+            for slot, m in enumerate(rows):
+                c = first_column(m) - VECTOR_ROWS
+                nc.tensor.matmul(out=totals[:, c:c + P], lhsT=turned[:, slot, :], rhs=ident[:], start=False, stop=False,
+                                 is_transpose=True)
+                rows_left[0] -= 1
+                i = row_slot + m - VECTOR_ROWS
+                nc.tensor.matmul(out=totals[:, i:i + 1], lhsT=turned[:, slot, :], rhs=(ones[:] if m < P else not_first[:]),
+                                 start=False, stop=(rows_left[0] == 0))
+
+        def finish_ready(before):
+            while ready and ready[0][1] < before:
+                finish(ready.pop(0)[0])
+
+        def hand_over(step):
+            job = new_job(GPSIMD_JOB, -2.0)
+            for m, pieces in waiting:
+                add_terms(job, m, pieces)
+            waiting.clear()
+            ready.append((job, step))
+
         v = 0
         i_s = 0
         i_g = 0
         step = 0
-        waiting = []
 
         with tc.manual_schedule():
-            for q in (4, 5, 6, 7, 0, 1, 2, 3):
-                transpose_f(q)
-            while v < len(visits) or i_s < len(scalar_chunks) or i_g < len(gpsimd_chunks):
+            totals = psum.tile([P, 4 * P], F32, name="totals", tag="bank%d" % (RING + JOB_BANKS))
+            for i in range(4):
+                nc.tensor.matmul(out=totals[:, i * P:(i + 1) * P], lhsT=zeros[:], rhs=ident[:], start=(i == 0), stop=False,
+                                 is_transpose=True)
+            while v < len(visits) or i_s < len(scalar_rows) or i_g < len(gpsimd_rows):
                 shares = []
                 if v < len(visits):
-                    shares.append((vector_done / vector_total, 0))
-                if i_s < len(scalar_chunks):
-                    shares.append((i_s / float(len(scalar_chunks)), 1))
-                if i_g < len(gpsimd_chunks):
-                    shares.append((i_g / float(len(gpsimd_chunks)), 2))
+                    shares.append((v / float(len(visits)), 0))
+                if i_s < len(scalar_rows):
+                    shares.append((i_s / float(len(scalar_rows)), 1))
+                if i_g < len(gpsimd_rows):
+                    shares.append((i_g / float(len(gpsimd_rows)), 2))
                 route = min(shares)[1]
                 step += 1
                 if route == 0:
@@ -382,37 +364,50 @@ def tile_minibatchdiscriminator_kernel(tc, tensor, T_bytes, T_scale, out):
                     add_columns(step - 1)
                     if visits[v][1] == EXP_LAG and visits[v][0] > 0:
                         vector_exp(visits[v][0] - 1, step)
-                    vector_done += visit_work[v]
+                    if i_s == len(scalar_rows):
+                        finish_ready(step)
                     v += 1
                 elif route == 1:
-                    chunk_step(scalar_terms(scalar_chunks[i_s]), step)
+                    m = scalar_rows[i_s]
+                    pieces = scalar_terms(m)
+                    if not open_job:
+                        open_job.append(new_job(SCALAR_JOB, -1.0))
+                    add_terms(open_job[0], m, pieces)
+                    finish_ready(step)
+                    if len(open_job[0][0]) == SCALAR_JOB or i_s == len(scalar_rows) - 1:
+                        ready.append((open_job.pop(0), step))
                     add_columns(step - 1)
                     i_s += 1
                 else:
-                    for made in waiting:
-                        chunk_step(made, step)
-                    waiting = [gpsimd_terms(gpsimd_chunks[i_g])]
+                    if i_s == len(scalar_rows):
+                        finish_ready(step)
+                    if len(waiting) == GPSIMD_JOB:
+                        hand_over(step)
+                    m = gpsimd_rows[i_g]
+                    waiting.append((m, gpsimd_terms(m)))
                     add_columns(step - 1)
                     i_g += 1
-            for made in waiting:
-                step += 1
-                chunk_step(made, step)
+            step += 1
+            if waiting:
+                hand_over(step)
             vector_exp(len(batches) - 1, step)
-            for i in range(2):
-                step += 1
-                chunk_step(None, step)
+            finish_ready(step + 1)
             add_columns(step + 1)
+
+        nc.scalar.copy(out=totals_sb[:, VECTOR_ROWS:EXT], in_=totals[:, 0:row_slot])
+        nc.vector.tensor_copy(out=row_sums[:, VECTOR_ROWS:ROWS], in_=totals[:, row_slot:row_slot + ROWS - VECTOR_ROWS])
 
         diversity = psum.tile([P, 2, P], F32, name="diversity", tag="bank0")
         for h in range(2):
             block = slice(h * P, (h + 1) * P)
-            for r in range(GROUP):
-                nc.tensor.matmul(out=diversity[:, h, :], lhsT=col_sums[:, r, block], rhs=ident[:], start=(r == 0), stop=False,
+            parts = [col_sums[:, r * PLANE + h * P:r * PLANE + (h + 1) * P] for r in range(GROUP)]
+            parts.append(totals_sb[:, block])
+            if h == 0:
+                parts.append(totals_sb[:, ROWS:EXT])
+            parts.append(row_sums[:, block])
+            for i, part in enumerate(parts):
+                nc.tensor.matmul(out=diversity[:, h, :], lhsT=part, rhs=ident[:], start=(i == 0), stop=(i == len(parts) - 1),
                                  is_transpose=True)
-            nc.tensor.matmul(out=diversity[:, h, :], lhsT=row_sums2[:, block], rhs=ident[:], start=False, stop=False,
-                             is_transpose=True)
-            nc.tensor.matmul(out=diversity[:, h, :], lhsT=row_sums[:, block], rhs=ident[:], start=False, stop=True,
-                             is_transpose=True)
         diversity_sb = keep.tile([P, 2, P], F32, name="diversity_sb")
         nc.vector.tensor_copy(out=diversity_sb[:], in_=diversity[:])
         nc.sync.dma_start(out=out[:, IN_F:IN_F + P].rearrange("(h p) j -> p h j", p=P), in_=diversity_sb[:])

@@ -26,14 +26,12 @@ PAIRS = KK // 2
 RING = 4
 JOB_BANKS = 3
 GROUP = 4
-BATCH = 16
-VECTOR_ROWS = 124
-SCALAR_ROWS = 92
+BATCH = 32
+VECTOR_ROWS = 128
+GPSIMD_ROWS = 24
 SCALAR_JOB = 4
-GPSIMD_JOB = 2
-EXP_LAG = 2
 BIG = 3.0e38
-PLANE = ROWS
+PLANE = EXT
 HALF = IN_F // 2
 VECTOR_COLS = 384
 
@@ -62,7 +60,7 @@ def tile_minibatchdiscriminator_kernel(tc, tensor, T_bytes, T_scale, out):
         nc.gpsimd.memset(ones[:], 1.0)
         not_first = keep.tile([P, 1], F32, name="not_first")
         nc.vector.tensor_scalar(out=not_first[:], in0=ident[:, 0:1], scalar1=-1.0, scalar2=1.0, op0=ALU.mult, op1=ALU.add)
-        col_sums = keep.tile([P, GROUP * (PLANE + 1) + P], F32, name="col_sums")
+        col_sums = keep.tile([P, GROUP * (PLANE + 1) + ROWS], F32, name="col_sums")
         nc.gpsimd.memset(col_sums[:], 0.0)
         nc.gpsimd.memset(col_sums[:, 0:P], 1.0)
         row_sums = keep.tile([P, ROWS], F32, name="row_sums")
@@ -213,28 +211,37 @@ def tile_minibatchdiscriminator_kernel(tc, tensor, T_bytes, T_scale, out):
                                 op1=ALU.add)
 
         acc_pool = ctx.enter_context(tc.tile_pool(name="acc_pool", bufs=2))
-        exp_pool = ctx.enter_context(tc.tile_pool(name="exp_pool", bufs=9))
+        exp_pool = ctx.enter_context(tc.tile_pool(name="exp_pool", bufs=8))
         term_pool = ctx.enter_context(tc.tile_pool(name="term_pool", bufs=4))
+        own_pool = ctx.enter_context(tc.tile_pool(name="own_pool", bufs=2))
         turned_pool = ctx.enter_context(tc.tile_pool(name="turned_pool", bufs=3))
 
         vector_groups = list(range(0, VECTOR_ROWS, GROUP))
         per_batch = BATCH // GROUP
         batches = [vector_groups[i:i + per_batch] for i in range(0, len(vector_groups), per_batch)]
         visits = [(b, q) for b in range(len(batches)) for q in range(PAIRS)]
-        scalar_rows = list(range(VECTOR_ROWS, VECTOR_ROWS + SCALAR_ROWS))
-        gpsimd_rows = list(range(VECTOR_ROWS + SCALAR_ROWS, ROWS))
-        row_slot = EXT - VECTOR_ROWS
-        rows_left = [ROWS - VECTOR_ROWS]
+        pieces_of = []
+        for number, (b, q) in enumerate(visits):
+            width = 2 if q == PAIRS - 1 else len(batches[b])
+            pieces_of.extend([(number, g0, min(g0 + width, len(batches[b]))) for g0 in range(0, len(batches[b]), width)])
+        vector_total = float(sum([g1 - g0 for number, g0, g1 in pieces_of]))
+        gpsimd_rows = list(range(VECTOR_ROWS, VECTOR_ROWS + GPSIMD_ROWS))
+        scalar_first = VECTOR_ROWS + GPSIMD_ROWS
+        scalar_rows = list(range(scalar_first, ROWS))
+        row_slot = EXT - scalar_first
+        rows_left = [len(scalar_rows)]
 
         ring = {}
         for v in range(RING):
             ring[v] = f_bank[v]
         acc_of = {}
+        fresh = {0: [], 2: []}
+        exps_due = []
         cols_due = []
         jobs = []
         open_job = []
         ready = []
-        waiting = []
+        own_sums = []
 
         def refill(v):
             q = visits[v][1]
@@ -244,7 +251,7 @@ def tile_minibatchdiscriminator_kernel(tc, tensor, T_bytes, T_scale, out):
                     nc.tensor.transpose(bank[:, s, h * P:(h + 1) * P], f_t[:, h, 2 * q + s, :], ident[:])
             ring[v] = bank
 
-        def vector_visit(v):
+        def vector_visit(v, g0, g1):
             b, q = visits[v]
             if q == 0:
                 acc_new = acc_pool.tile([P, BATCH, P], F32, name="acc", tag="acc")
@@ -252,10 +259,10 @@ def tile_minibatchdiscriminator_kernel(tc, tensor, T_bytes, T_scale, out):
             acc = acc_of[b]
             for s in range(2):
                 k = 2 * q + s
-                for gi, m0 in enumerate(batches[b]):
+                for gi in range(g0, g1):
                     for r in range(GROUP):
                         row = gi * GROUP + r
-                        m = m0 + r
+                        m = batches[b][gi] + r
                         c = first_column(m)
                         nc.vector.scalar_tensor_tensor(
                             out=acc[:, row, :],
@@ -265,21 +272,30 @@ def tile_minibatchdiscriminator_kernel(tc, tensor, T_bytes, T_scale, out):
                             op0=ALU.max,
                             op1=ALU.add,
                         )
+            if q == PAIRS - 1:
+                for gi in range(g0, g1):
+                    fresh[0].append((acc[:, gi * GROUP:(gi + 1) * GROUP, :], batches[b][gi]))
 
-        def vector_exp(b, step):
-            for gi, m0 in enumerate(batches[b]):
+        def release(route):
+            exps_due.extend(fresh[route])
+            fresh[route].clear()
+
+        def group_exp(step):
+            if exps_due:
+                sums, m0 = exps_due.pop(0)
                 e = exp_pool.tile([P, GROUP, P], F32, name="e", tag="e")
                 for r in range(GROUP):
                     m = m0 + r
-                    nc.scalar.activation(out=e[:, r, :], in_=acc_of[b][:, gi * GROUP + r, :], func=ACT.Exp,
-                                         bias=s_sum[:, m:m + 1], scale=-2.0, accum_out=row_sums[:, m:m + 1])
+                    nc.scalar.activation(out=e[:, r, :], in_=sums[:, r, :], func=ACT.Exp, bias=s_sum[:, m:m + 1], scale=-2.0,
+                                         accum_out=row_sums[:, m:m + 1])
                 cols_due.append((e, m0, step))
 
         def add_columns(before):
             while cols_due and cols_due[0][2] < before:
                 e, m0, issued = cols_due.pop(0)
-                slanted = col_sums[:, m0 + 1:m0 + 1 + GROUP * (PLANE + 1)].rearrange("p (r w) -> p r w", w=PLANE + 1)[:, :, 0:P]
-                nc.gpsimd.tensor_tensor(out=slanted, in0=slanted, in1=e[:], op=ALU.add)
+                skip = m0 + 1 - first_column(m0)
+                slanted = col_sums[:, m0 + 1:m0 + 1 + GROUP * (PLANE + 1)].rearrange("p (r w) -> p r w", w=PLANE + 1)[:, :, 0:P - skip]
+                nc.gpsimd.tensor_tensor(out=slanted, in0=slanted, in1=e[:, :, skip:P], op=ALU.add)
 
         def scalar_terms(m):
             terms = term_pool.tile([P, KK, P], F32, name="abs_terms", tag="abs_terms")
@@ -289,20 +305,28 @@ def tile_minibatchdiscriminator_kernel(tc, tensor, T_bytes, T_scale, out):
                                      scale=-1.0)
             return [terms[:, k, :] for k in range(KK)]
 
-        def gpsimd_terms(m):
-            terms = term_pool.tile([P, KK, P], F32, name="max_terms", tag="max_terms")
+        def gpsimd_row(m, step):
+            terms = own_pool.tile([P, KK, P], F32, name="max_terms", tag="max_terms")
             c = first_column(m)
             for k in range(KK):
                 nc.gpsimd.tensor_scalar(out=terms[:, k, :], in0=f_ext[:, k, c:c + P], scalar1=BIG, scalar2=f_ext[:, k, m:m + 1],
                                         op0=ALU.min, op1=ALU.max)
-            s_term = term_pool.tile([P, P], F32, name="s_term", tag="s_term")
-            nc.vector.tensor_scalar(out=s_term[:], in0=minus_half_s[:, c:c + P], scalar1=minus_half_s[:, m:m + 1], scalar2=None,
-                                    op0=ALU.add)
-            return [terms[:, k, :] for k in range(KK)] + [s_term[:]]
+            half = KK // 2
+            while half >= 1:
+                nc.gpsimd.tensor_tensor(out=terms[:, 0:half, :], in0=terms[:, 0:half, :], in1=terms[:, half:2 * half, :], op=ALU.add)
+                half //= 2
+            r = (m - VECTOR_ROWS) % GROUP
+            if r == 0:
+                sums_new = own_pool.tile([P, GROUP, P], F32, name="own_sums", tag="own_sums")
+                own_sums.clear()
+                own_sums.append(sums_new)
+            nc.gpsimd.tensor_tensor(out=own_sums[0][:, r, :], in0=terms[:, 0, :], in1=minus_half_s[:, c:c + P], op=ALU.add)
+            if r == GROUP - 1:
+                fresh[2].append((own_sums[0][:], m - r))
 
-        def new_job(size, scale):
-            bank = psum.tile([P, size, P], F32, name="job", tag="bank%d" % (RING + len(jobs) % JOB_BANKS))
-            job = [[], bank, scale]
+        def new_job():
+            bank = psum.tile([P, SCALAR_JOB, P], F32, name="job", tag="bank%d" % (RING + len(jobs) % JOB_BANKS))
+            job = [[], bank]
             jobs.append(job)
             return job
 
@@ -314,15 +338,15 @@ def tile_minibatchdiscriminator_kernel(tc, tensor, T_bytes, T_scale, out):
                                  is_transpose=True)
 
         def finish(job):
-            rows, bank, scale = job
+            rows, bank = job
             turned = turned_pool.tile([P, SCALAR_JOB, P], F32, name="turned", tag="turned")
-            nc.scalar.activation(out=turned[:, 0:len(rows), :], in_=bank[:, 0:len(rows), :], func=ACT.Exp, scale=scale)
+            nc.scalar.activation(out=turned[:, 0:len(rows), :], in_=bank[:, 0:len(rows), :], func=ACT.Exp, scale=-1.0)
             for slot, m in enumerate(rows):
-                c = first_column(m) - VECTOR_ROWS
+                c = first_column(m) - scalar_first
                 nc.tensor.matmul(out=totals[:, c:c + P], lhsT=turned[:, slot, :], rhs=ident[:], start=False, stop=False,
                                  is_transpose=True)
                 rows_left[0] -= 1
-                i = row_slot + m - VECTOR_ROWS
+                i = row_slot + m - scalar_first
                 nc.tensor.matmul(out=totals[:, i:i + 1], lhsT=turned[:, slot, :], rhs=(ones[:] if m < P else not_first[:]),
                                  start=False, stop=(rows_left[0] == 0))
 
@@ -330,14 +354,8 @@ def tile_minibatchdiscriminator_kernel(tc, tensor, T_bytes, T_scale, out):
             while ready and ready[0][1] < before:
                 finish(ready.pop(0)[0])
 
-        def hand_over(step):
-            job = new_job(GPSIMD_JOB, -2.0)
-            for m, pieces in waiting:
-                add_terms(job, m, pieces)
-            waiting.clear()
-            ready.append((job, step))
-
-        v = 0
+        i_v = 0
+        vector_done = 0
         i_s = 0
         i_g = 0
         step = 0
@@ -347,10 +365,10 @@ def tile_minibatchdiscriminator_kernel(tc, tensor, T_bytes, T_scale, out):
             for i in range(4):
                 nc.tensor.matmul(out=totals[:, i * P:(i + 1) * P], lhsT=zeros[:], rhs=ident[:], start=(i == 0), stop=False,
                                  is_transpose=True)
-            while v < len(visits) or i_s < len(scalar_rows) or i_g < len(gpsimd_rows):
+            while i_v < len(pieces_of) or i_s < len(scalar_rows) or i_g < len(gpsimd_rows):
                 shares = []
-                if v < len(visits):
-                    shares.append((v / float(len(visits)), 0))
+                if i_v < len(pieces_of):
+                    shares.append((vector_done / vector_total, 0))
                 if i_s < len(scalar_rows):
                     shares.append((i_s / float(len(scalar_rows)), 1))
                 if i_g < len(gpsimd_rows):
@@ -358,52 +376,51 @@ def tile_minibatchdiscriminator_kernel(tc, tensor, T_bytes, T_scale, out):
                 route = min(shares)[1]
                 step += 1
                 if route == 0:
-                    vector_visit(v)
-                    if RING <= v + 2 < len(visits):
+                    release(0)
+                    v, g0, g1 = pieces_of[i_v]
+                    vector_visit(v, g0, g1)
+                    if g0 == 0 and RING <= v + 2 < len(visits):
                         refill(v + 2)
-                    add_columns(step - 1)
-                    if visits[v][1] == EXP_LAG and visits[v][0] > 0:
-                        vector_exp(visits[v][0] - 1, step)
-                    if i_s == len(scalar_rows):
-                        finish_ready(step)
-                    v += 1
+                    vector_done += g1 - g0
+                    i_v += 1
                 elif route == 1:
                     m = scalar_rows[i_s]
                     pieces = scalar_terms(m)
                     if not open_job:
-                        open_job.append(new_job(SCALAR_JOB, -1.0))
+                        open_job.append(new_job())
                     add_terms(open_job[0], m, pieces)
                     finish_ready(step)
                     if len(open_job[0][0]) == SCALAR_JOB or i_s == len(scalar_rows) - 1:
                         ready.append((open_job.pop(0), step))
-                    add_columns(step - 1)
+                    group_exp(step)
                     i_s += 1
                 else:
-                    if i_s == len(scalar_rows):
-                        finish_ready(step)
-                    if len(waiting) == GPSIMD_JOB:
-                        hand_over(step)
-                    m = gpsimd_rows[i_g]
-                    waiting.append((m, gpsimd_terms(m)))
-                    add_columns(step - 1)
+                    release(2)
+                    gpsimd_row(gpsimd_rows[i_g], step)
                     i_g += 1
+                if i_s == len(scalar_rows):
+                    finish_ready(step)
+                    group_exp(step)
+                add_columns(step - 1)
             step += 1
-            if waiting:
-                hand_over(step)
-            vector_exp(len(batches) - 1, step)
-            finish_ready(step + 1)
+            finish_ready(step)
+            release(0)
+            release(2)
+            while exps_due:
+                group_exp(step)
             add_columns(step + 1)
 
-        nc.scalar.copy(out=totals_sb[:, VECTOR_ROWS:EXT], in_=totals[:, 0:row_slot])
-        nc.vector.tensor_copy(out=row_sums[:, VECTOR_ROWS:ROWS], in_=totals[:, row_slot:row_slot + ROWS - VECTOR_ROWS])
+        nc.scalar.copy(out=totals_sb[:, scalar_first:EXT], in_=totals[:, 0:row_slot])
+        nc.vector.tensor_copy(out=row_sums[:, scalar_first:ROWS], in_=totals[:, row_slot:row_slot + ROWS - scalar_first])
 
         diversity = psum.tile([P, 2, P], F32, name="diversity", tag="bank0")
         for h in range(2):
             block = slice(h * P, (h + 1) * P)
             parts = [col_sums[:, r * PLANE + h * P:r * PLANE + (h + 1) * P] for r in range(GROUP)]
-            parts.append(totals_sb[:, block])
             if h == 0:
+                parts.extend([col_sums[:, r * PLANE + ROWS:r * PLANE + EXT] for r in range(GROUP)])
                 parts.append(totals_sb[:, ROWS:EXT])
+            parts.append(totals_sb[:, block])
             parts.append(row_sums[:, block])
             for i, part in enumerate(parts):
                 nc.tensor.matmul(out=diversity[:, h, :], lhsT=part, rhs=ident[:], start=(i == 0), stop=(i == len(parts) - 1),

@@ -28,10 +28,10 @@ JOB_BANKS = 3
 GROUP = 4
 BATCH = 32
 VECTOR_ROWS = 128
-GPSIMD_ROWS = 24
+GPSIMD_ROWS = 20
 SCALAR_JOB = 4
 BIG = 3.0e38
-PLANE = EXT
+PLANE = EXT + GROUP
 HALF = IN_F // 2
 VECTOR_COLS = 384
 
@@ -40,6 +40,10 @@ def first_column(m):
     if m < P:
         return m + 1
     return m
+
+
+def own_pair(m):
+    return m + 1 - first_column(m)
 
 
 def tile_minibatchdiscriminator_kernel(tc, tensor, T_bytes, T_scale, out):
@@ -60,9 +64,9 @@ def tile_minibatchdiscriminator_kernel(tc, tensor, T_bytes, T_scale, out):
         nc.gpsimd.memset(ones[:], 1.0)
         not_first = keep.tile([P, 1], F32, name="not_first")
         nc.vector.tensor_scalar(out=not_first[:], in0=ident[:, 0:1], scalar1=-1.0, scalar2=1.0, op0=ALU.mult, op1=ALU.add)
-        col_sums = keep.tile([P, GROUP * (PLANE + 1) + ROWS], F32, name="col_sums")
+        col_sums = keep.tile([P, GROUP, PLANE], F32, name="col_sums")
         nc.gpsimd.memset(col_sums[:], 0.0)
-        nc.gpsimd.memset(col_sums[:, 0:P], 1.0)
+        nc.gpsimd.memset(col_sums[:, 0, GROUP - 1:GROUP - 1 + P], 1.0)
         row_sums = keep.tile([P, ROWS], F32, name="row_sums")
         totals_sb = keep.tile([P, EXT], F32, name="totals_sb")
         nc.gpsimd.memset(totals_sb[:], 0.0)
@@ -283,19 +287,20 @@ def tile_minibatchdiscriminator_kernel(tc, tensor, T_bytes, T_scale, out):
         def group_exp(step):
             if exps_due:
                 sums, m0 = exps_due.pop(0)
-                e = exp_pool.tile([P, GROUP, P], F32, name="e", tag="e")
+                e = exp_pool.tile([P, GROUP, P + GROUP], F32, name="e", tag="e")
+                lead = own_pair(m0) * (GROUP - 1)
                 for r in range(GROUP):
                     m = m0 + r
-                    nc.scalar.activation(out=e[:, r, :], in_=sums[:, r, :], func=ACT.Exp, bias=s_sum[:, m:m + 1], scale=-2.0,
+                    nc.scalar.activation(out=e[:, r, lead:lead + P], in_=sums[:, r, :], func=ACT.Exp, bias=s_sum[:, m:m + 1], scale=-2.0,
                                          accum_out=row_sums[:, m:m + 1])
                 cols_due.append((e, m0, step))
 
         def add_columns(before):
             while cols_due and cols_due[0][2] < before:
                 e, m0, issued = cols_due.pop(0)
-                skip = m0 + 1 - first_column(m0)
-                slanted = col_sums[:, m0 + 1:m0 + 1 + GROUP * (PLANE + 1)].rearrange("p (r w) -> p r w", w=PLANE + 1)[:, :, 0:P - skip]
-                nc.gpsimd.tensor_tensor(out=slanted, in0=slanted, in1=e[:, :, skip:P], op=ALU.add)
+                skip = own_pair(m0)
+                target = col_sums[:, :, m0 + GROUP:m0 + GROUP + P - skip]
+                nc.gpsimd.tensor_tensor(out=target, in0=target, in1=e[:, :, GROUP * skip:GROUP * skip + P - skip], op=ALU.add)
 
         def scalar_terms(m):
             terms = term_pool.tile([P, KK, P], F32, name="abs_terms", tag="abs_terms")
@@ -416,9 +421,9 @@ def tile_minibatchdiscriminator_kernel(tc, tensor, T_bytes, T_scale, out):
         diversity = psum.tile([P, 2, P], F32, name="diversity", tag="bank0")
         for h in range(2):
             block = slice(h * P, (h + 1) * P)
-            parts = [col_sums[:, r * PLANE + h * P:r * PLANE + (h + 1) * P] for r in range(GROUP)]
+            parts = [col_sums[:, r, GROUP - 1 - r + h * P:GROUP - 1 - r + (h + 1) * P] for r in range(GROUP)]
             if h == 0:
-                parts.extend([col_sums[:, r * PLANE + ROWS:r * PLANE + EXT] for r in range(GROUP)])
+                parts.extend([col_sums[:, r, GROUP - 1 - r + ROWS:GROUP - 1 - r + EXT] for r in range(GROUP)])
                 parts.append(totals_sb[:, ROWS:EXT])
             parts.append(totals_sb[:, block])
             parts.append(row_sums[:, block])

@@ -28,7 +28,7 @@ JOB_BANKS = 3
 GROUP = 4
 BATCH = 32
 VECTOR_ROWS = 128
-GPSIMD_ROWS = 20
+GPSIMD_ROWS = 22
 SCALAR_JOB = 4
 BIG = 3.0e38
 PLANE = EXT + GROUP
@@ -289,17 +289,17 @@ def tile_minibatchdiscriminator_kernel(tc, tensor, T_bytes, T_scale, out):
                 sums, m0 = exps_due.pop(0)
                 e = exp_pool.tile([P, GROUP, P + GROUP], F32, name="e", tag="e")
                 lead = own_pair(m0) * (GROUP - 1)
-                for r in range(GROUP):
+                for r in range(sums.shape[1]):
                     m = m0 + r
                     nc.scalar.activation(out=e[:, r, lead:lead + P], in_=sums[:, r, :], func=ACT.Exp, bias=s_sum[:, m:m + 1], scale=-2.0,
                                          accum_out=row_sums[:, m:m + 1])
-                cols_due.append((e, m0, step))
+                cols_due.append((e[:, 0:sums.shape[1], :], m0, step))
 
         def add_columns(before):
             while cols_due and cols_due[0][2] < before:
                 e, m0, issued = cols_due.pop(0)
                 skip = own_pair(m0)
-                target = col_sums[:, :, m0 + GROUP:m0 + GROUP + P - skip]
+                target = col_sums[:, 0:e.shape[1], m0 + GROUP:m0 + GROUP + P - skip]
                 nc.gpsimd.tensor_tensor(out=target, in0=target, in1=e[:, :, GROUP * skip:GROUP * skip + P - skip], op=ALU.add)
 
         def scalar_terms(m):
@@ -326,8 +326,8 @@ def tile_minibatchdiscriminator_kernel(tc, tensor, T_bytes, T_scale, out):
                 own_sums.clear()
                 own_sums.append(sums_new)
             nc.gpsimd.tensor_tensor(out=own_sums[0][:, r, :], in0=terms[:, 0, :], in1=minus_half_s[:, c:c + P], op=ALU.add)
-            if r == GROUP - 1:
-                fresh[2].append((own_sums[0][:], m - r))
+            if r == GROUP - 1 or m == gpsimd_rows[-1]:
+                fresh[2].append((own_sums[0][:, 0:r + 1, :], m - r))
 
         def new_job():
             bank = psum.tile([P, SCALAR_JOB, P], F32, name="job", tag="bank%d" % (RING + len(jobs) % JOB_BANKS))

@@ -116,8 +116,8 @@ def tile_minibatchdiscriminator_kernel(tc, tensor, T_bytes, T_scale, out):
                                             scalar1=t_scale[:, g, t:t + 1], scalar2=None, op0=ALU.mult)
 
             def interleave(g, half, c0, c1, on_scalar):
-                dst = grouped_of[(g, half)][:].rearrange("p (c t) -> p c t", t=PACK)[:, c0:c1, :]
-                src = widened[g][:, :, half * HALF + c0:half * HALF + c1].rearrange("p t c -> p c t")
+                dst = grouped_of[(g, half)][:, c0 * PACK:c1 * PACK].rearrange("p (c i t) -> p c t i", i=4, t=PACK)
+                src = widened[g][:, :, half * HALF + c0:half * HALF + c1].rearrange("p t (c i) -> p c t i", i=4)
                 if on_scalar:
                     nc.scalar.copy(out=dst, in_=src)
                 else:

@@ -28,10 +28,11 @@ JOB_BANKS = 3
 GROUP = 4
 BATCH = 32
 VECTOR_ROWS = 128
-GPSIMD_ROWS = 22
+GPSIMD_ROWS = 24
 SCALAR_JOB = 4
 BIG = 3.0e38
 PLANE = EXT + GROUP
+SLANTED = GPSIMD_ROWS + GROUP + P
 HALF = IN_F // 2
 VECTOR_COLS = 384
 
@@ -76,6 +77,7 @@ def tile_minibatchdiscriminator_kernel(tc, tensor, T_bytes, T_scale, out):
         s_t = keep.tile([P, 2, P], F32, name="s_t")
         s_sum = keep.tile([P, ROWS], F32, name="s_sum")
         minus_half_s = keep.tile([P, EXT], F32, name="minus_half_s")
+        minus_half_s_slanted = keep.tile([P, GROUP, SLANTED], F32, name="minus_half_s_slanted")
         f_bank = []
 
         with ExitStack() as head:
@@ -210,6 +212,8 @@ def tile_minibatchdiscriminator_kernel(tc, tensor, T_bytes, T_scale, out):
                 nc.vector.tensor_copy(out=s_sum[:], in_=s_bank[:])
                 nc.vector.tensor_scalar(out=minus_half_s[:, 0:ROWS], in0=s_sum[:], scalar1=-0.5, scalar2=None, op0=ALU.mult)
                 nc.vector.tensor_scalar(out=minus_half_s[:, ROWS:EXT], in0=s_sum[:, 0:P], scalar1=-0.5, scalar2=None, op0=ALU.mult)
+                for r in range(GROUP):
+                    nc.vector.tensor_copy(out=minus_half_s_slanted[:, r, :], in_=minus_half_s[:, VECTOR_ROWS + r:VECTOR_ROWS + r + SLANTED])
 
         nc.gpsimd.tensor_scalar(out=f_ext[:, :, ROWS:EXT], in0=f_ext[:, :, 0:P], scalar1=1.0, scalar2=0.0, op0=ALU.mult,
                                 op1=ALU.add)
@@ -229,7 +233,13 @@ def tile_minibatchdiscriminator_kernel(tc, tensor, T_bytes, T_scale, out):
             width = 2 if q == PAIRS - 1 else len(batches[b])
             pieces_of.extend([(number, g0, min(g0 + width, len(batches[b]))) for g0 in range(0, len(batches[b]), width)])
         vector_total = float(sum([g1 - g0 for number, g0, g1 in pieces_of]))
-        gpsimd_rows = list(range(VECTOR_ROWS, VECTOR_ROWS + GPSIMD_ROWS))
+        gpsimd_pieces = []
+        for m0 in range(VECTOR_ROWS, VECTOR_ROWS + GPSIMD_ROWS, GROUP):
+            n = min(GROUP, VECTOR_ROWS + GPSIMD_ROWS - m0)
+            gpsimd_pieces.extend([("row", m0 + r, 0, KK * P) for r in range(n)])
+            gpsimd_pieces.extend([("halve", n, half, n * half * P) for half in (8, 4, 2, 1)])
+            gpsimd_pieces.append(("last", m0, n, n * P))
+        gpsimd_total = float(sum([piece[3] for piece in gpsimd_pieces]))
         scalar_first = VECTOR_ROWS + GPSIMD_ROWS
         scalar_rows = list(range(scalar_first, ROWS))
         row_slot = EXT - scalar_first
@@ -245,7 +255,7 @@ def tile_minibatchdiscriminator_kernel(tc, tensor, T_bytes, T_scale, out):
         jobs = []
         open_job = []
         ready = []
-        own_sums = []
+        own_terms = []
 
         def refill(v):
             q = visits[v][1]
@@ -310,24 +320,28 @@ def tile_minibatchdiscriminator_kernel(tc, tensor, T_bytes, T_scale, out):
                                      scale=-1.0)
             return [terms[:, k, :] for k in range(KK)]
 
-        def gpsimd_row(m, step):
-            terms = own_pool.tile([P, KK, P], F32, name="max_terms", tag="max_terms")
-            c = first_column(m)
-            for k in range(KK):
-                nc.gpsimd.tensor_scalar(out=terms[:, k, :], in0=f_ext[:, k, c:c + P], scalar1=BIG, scalar2=f_ext[:, k, m:m + 1],
-                                        op0=ALU.min, op1=ALU.max)
-            half = KK // 2
-            while half >= 1:
-                nc.gpsimd.tensor_tensor(out=terms[:, 0:half, :], in0=terms[:, 0:half, :], in1=terms[:, half:2 * half, :], op=ALU.add)
-                half //= 2
+        def gpsimd_row(m):
             r = (m - VECTOR_ROWS) % GROUP
             if r == 0:
-                sums_new = own_pool.tile([P, GROUP, P], F32, name="own_sums", tag="own_sums")
-                own_sums.clear()
-                own_sums.append(sums_new)
-            nc.gpsimd.tensor_tensor(out=own_sums[0][:, r, :], in0=terms[:, 0, :], in1=minus_half_s[:, c:c + P], op=ALU.add)
-            if r == GROUP - 1 or m == gpsimd_rows[-1]:
-                fresh[2].append((own_sums[0][:, 0:r + 1, :], m - r))
+                terms_new = own_pool.tile([P, GROUP, KK, P], F32, name="max_terms", tag="max_terms", bufs=1)
+                own_terms.clear()
+                own_terms.append(terms_new)
+            c = first_column(m)
+            for k in range(KK):
+                nc.gpsimd.tensor_scalar(out=own_terms[0][:, r, k, :], in0=f_ext[:, k, c:c + P], scalar1=BIG,
+                                        scalar2=f_ext[:, k, m:m + 1], op0=ALU.min, op1=ALU.max)
+
+        def gpsimd_halve(n, half):
+            terms = own_terms[0]
+            nc.gpsimd.tensor_tensor(out=terms[:, 0:n, 0:half, :], in0=terms[:, 0:n, 0:half, :], in1=terms[:, 0:n, half:2 * half, :],
+                                    op=ALU.add)
+
+        def gpsimd_last(m0, n):
+            sums = own_pool.tile([P, GROUP, P], F32, name="own_sums", tag="own_sums")
+            c0 = first_column(m0) - VECTOR_ROWS
+            nc.gpsimd.tensor_tensor(out=sums[:, 0:n, :], in0=own_terms[0][:, 0:n, 0, :], in1=minus_half_s_slanted[:, 0:n, c0:c0 + P],
+                                    op=ALU.add)
+            fresh[2].append((sums[:, 0:n, :], m0))
 
         def new_job():
             bank = psum.tile([P, SCALAR_JOB, P], F32, name="job", tag="bank%d" % (RING + len(jobs) % JOB_BANKS))
@@ -363,6 +377,7 @@ def tile_minibatchdiscriminator_kernel(tc, tensor, T_bytes, T_scale, out):
         vector_done = 0
         i_s = 0
         i_g = 0
+        gpsimd_done = 0
         step = 0
 
         with tc.manual_schedule():
@@ -370,14 +385,14 @@ def tile_minibatchdiscriminator_kernel(tc, tensor, T_bytes, T_scale, out):
             for i in range(4):
                 nc.tensor.matmul(out=totals[:, i * P:(i + 1) * P], lhsT=zeros[:], rhs=ident[:], start=(i == 0), stop=False,
                                  is_transpose=True)
-            while i_v < len(pieces_of) or i_s < len(scalar_rows) or i_g < len(gpsimd_rows):
+            while i_v < len(pieces_of) or i_s < len(scalar_rows) or i_g < len(gpsimd_pieces):
                 shares = []
                 if i_v < len(pieces_of):
                     shares.append((vector_done / vector_total, 0))
                 if i_s < len(scalar_rows):
                     shares.append((i_s / float(len(scalar_rows)), 1))
-                if i_g < len(gpsimd_rows):
-                    shares.append((i_g / float(len(gpsimd_rows)), 2))
+                if i_g < len(gpsimd_pieces):
+                    shares.append((gpsimd_done / gpsimd_total, 2))
                 route = min(shares)[1]
                 step += 1
                 if route == 0:
@@ -401,7 +416,14 @@ def tile_minibatchdiscriminator_kernel(tc, tensor, T_bytes, T_scale, out):
                     i_s += 1
                 else:
                     release(2)
-                    gpsimd_row(gpsimd_rows[i_g], step)
+                    kind, first, second, elements = gpsimd_pieces[i_g]
+                    if kind == "row":
+                        gpsimd_row(first)
+                    elif kind == "halve":
+                        gpsimd_halve(first, second)
+                    else:
+                        gpsimd_last(first, second)
+                    gpsimd_done += elements
                     i_g += 1
                 if i_s == len(scalar_rows):
                     finish_ready(step)

@@ -409,10 +409,10 @@ def tile_minibatchdiscriminator_kernel(tc, tensor, T_bytes, T_scale, out):
                     if not open_job:
                         open_job.append(new_job())
                     add_terms(open_job[0], m, pieces)
-                    finish_ready(step)
-                    if len(open_job[0][0]) == SCALAR_JOB or i_s == len(scalar_rows) - 1:
-                        ready.append((open_job.pop(0), step))
                     group_exp(step)
+                    finish_ready(i_s - 1)
+                    if len(open_job[0][0]) == SCALAR_JOB or i_s == len(scalar_rows) - 1:
+                        ready.append((open_job.pop(0), i_s))
                     i_s += 1
                 else:
                     release(2)
@@ -426,15 +426,15 @@ def tile_minibatchdiscriminator_kernel(tc, tensor, T_bytes, T_scale, out):
                     gpsimd_done += elements
                     i_g += 1
                 if i_s == len(scalar_rows):
-                    finish_ready(step)
                     group_exp(step)
+                    finish_ready(i_s)
                 add_columns(step - 1)
             step += 1
-            finish_ready(step)
             release(0)
             release(2)
             while exps_due:
                 group_exp(step)
+            finish_ready(i_s)
             add_columns(step + 1)
 
         nc.scalar.copy(out=totals_sb[:, scalar_first:EXT], in_=totals[:, 0:row_slot])

@@ -34,6 +34,8 @@ BIG = 3.0e38
 PLANE = EXT + GROUP
 SLANTED = GPSIMD_ROWS + GROUP + P
 HALF = IN_F // 2
+VECTOR_CLOSING = 3
+VECTOR_BANKS = [3, 6]
 VECTOR_COLS = 384
 
 
@@ -92,8 +94,9 @@ def tile_minibatchdiscriminator_kernel(tc, tensor, T_bytes, T_scale, out):
             t_bytes = []
             for g in range(PASSES):
                 tb = bytes_pool.tile([P, PACK * IN_F], U8, name="t_bytes%d" % g)
-                for piece in range(2):
-                    run = slice(piece * 4096, (piece + 1) * 4096)
+                pieces = PACK if g == 0 else 2
+                for piece in range(pieces):
+                    run = slice(piece * PACK * IN_F // pieces, (piece + 1) * PACK * IN_F // pieces)
                     nc.sync.dma_start(out=tb[:, run], in_=bytes_view[g][:, run])
                 t_bytes.append(tb)
                 if g == 0:
@@ -184,39 +187,54 @@ def tile_minibatchdiscriminator_kernel(tc, tensor, T_bytes, T_scale, out):
                 for half in (1, 0):
                     quantize(PASSES - 1, half)
                     multiply(PASSES - 1, half)
-                for h in range(2):
-                    nc.vector.tensor_copy(out=x_f32[:, h, :], in_=x_sb[:, h, :])
-                    nc.sync.dma_start(out=out_x[:, h, :], in_=x_f32[:, h, :])
-
                 closing = [(h, cb) for cb in (2, 3, 0, 1) for h in range(2)]
                 for i, (h, cb) in enumerate(closing):
                     dst = f_t[:, h, :, cb * 32:(cb + 1) * 32]
                     src = ft_bank[(h, cb)][:].rearrange("p (j k) -> p k j", k=KK)
-                    if i < len(closing) - 2:
+                    if i < len(closing) - VECTOR_CLOSING:
                         nc.scalar.copy(out=dst, in_=src)
                     else:
                         nc.vector.tensor_copy(out=dst, in_=src)
-                for h, cb in closing:
-                    nc.vector.tensor_reduce(out=s_t[:, h, cb * 32:(cb + 1) * 32],
-                                            in_=f_t[:, h, :, cb * 32:(cb + 1) * 32].rearrange("p k j -> p j k"), axis=AX.X, op=ALU.add)
+
+                tree = stage.tile([P, 2, KK // 2, P], F32, name="tree", tag="w")
+
+                def halve(h, half):
+                    if half == KK // 2:
+                        nc.vector.tensor_tensor(out=tree[:, h, :, :], in0=f_t[:, h, 0:half, :], in1=f_t[:, h, half:2 * half, :], op=ALU.add)
+                    elif half > 1:
+                        nc.vector.tensor_tensor(out=tree[:, h, 0:half, :], in0=tree[:, h, 0:half, :], in1=tree[:, h, half:2 * half, :], op=ALU.add)
+                    else:
+                        nc.vector.tensor_tensor(out=s_t[:, h, :], in0=tree[:, h, 0, :], in1=tree[:, h, 1, :], op=ALU.add)
+
                 for q in range(PAIRS):
                     bank = psum.tile([P, 2, ROWS], F32, name="f_bank%d" % q, tag="bank%d" % q)
                     f_bank.append(bank)
                     for s in range(2):
                         for h in range(2):
                             nc.tensor.transpose(bank[:, s, h * P:(h + 1) * P], f_t[:, h, 2 * q + s, :], ident[:])
-                    nc.scalar.copy(out=f_ext[:, 2 * q:2 * q + 2, 0:ROWS], in_=bank[:])
+                    if q in VECTOR_BANKS:
+                        halve(VECTOR_BANKS.index(q), KK // 2)
+                        nc.vector.tensor_copy(out=f_ext[:, 2 * q:2 * q + 2, 0:ROWS], in_=bank[:])
+                    else:
+                        nc.scalar.copy(out=f_ext[:, 2 * q:2 * q + 2, 0:ROWS], in_=bank[:])
+                    if q % 2 == 1:
+                        nc.gpsimd.tensor_scalar(out=f_ext[:, 2 * q - 2:2 * q + 2, ROWS:EXT], in0=f_ext[:, 2 * q - 2:2 * q + 2, 0:P], scalar1=1.0,
+                                                scalar2=0.0, op0=ALU.mult, op1=ALU.add)
+                for half in (4, 2, 1):
+                    for h in range(2):
+                        halve(h, half)
                 s_bank = psum.tile([P, ROWS], F32, name="s_bank", tag="bank7")
                 for h in range(2):
                     nc.tensor.transpose(s_bank[:, h * P:(h + 1) * P], s_t[:, h, :], ident[:])
+                for h in range(2):
+                    nc.vector.tensor_copy(out=x_f32[:, h, :], in_=x_sb[:, h, :])
+                    nc.sync.dma_start(out=out_x[:, h, :], in_=x_f32[:, h, :])
                 nc.vector.tensor_copy(out=s_sum[:], in_=s_bank[:])
                 nc.vector.tensor_scalar(out=minus_half_s[:, 0:ROWS], in0=s_sum[:], scalar1=-0.5, scalar2=None, op0=ALU.mult)
                 nc.vector.tensor_scalar(out=minus_half_s[:, ROWS:EXT], in0=s_sum[:, 0:P], scalar1=-0.5, scalar2=None, op0=ALU.mult)
                 for r in range(GROUP):
                     nc.vector.tensor_copy(out=minus_half_s_slanted[:, r, :], in_=minus_half_s[:, VECTOR_ROWS + r:VECTOR_ROWS + r + SLANTED])
 
-        nc.gpsimd.tensor_scalar(out=f_ext[:, :, ROWS:EXT], in0=f_ext[:, :, 0:P], scalar1=1.0, scalar2=0.0, op0=ALU.mult,
-                                op1=ALU.add)
 
         acc_pool = ctx.enter_context(tc.tile_pool(name="acc_pool", bufs=2))
         exp_pool = ctx.enter_context(tc.tile_pool(name="exp_pool", bufs=8))
@@ -443,12 +461,11 @@ def tile_minibatchdiscriminator_kernel(tc, tensor, T_bytes, T_scale, out):
         diversity = psum.tile([P, 2, P], F32, name="diversity", tag="bank0")
         for h in range(2):
             block = slice(h * P, (h + 1) * P)
-            parts = [col_sums[:, r, GROUP - 1 - r + h * P:GROUP - 1 - r + (h + 1) * P] for r in range(GROUP)]
+            parts = [row_sums[:, block], totals_sb[:, block]]
             if h == 0:
-                parts.extend([col_sums[:, r, GROUP - 1 - r + ROWS:GROUP - 1 - r + EXT] for r in range(GROUP)])
                 parts.append(totals_sb[:, ROWS:EXT])
-            parts.append(totals_sb[:, block])
-            parts.append(row_sums[:, block])
+                parts.extend([col_sums[:, r, GROUP - 1 - r + ROWS:GROUP - 1 - r + EXT] for r in range(GROUP)])
+            parts.extend([col_sums[:, r, GROUP - 1 - r + h * P:GROUP - 1 - r + (h + 1) * P] for r in range(GROUP)])
             for i, part in enumerate(parts):
                 nc.tensor.matmul(out=diversity[:, h, :], lhsT=part, rhs=ident[:], start=(i == 0), stop=(i == len(parts) - 1),
                                  is_transpose=True)

@@ -90,7 +90,7 @@ def tile_minibatchdiscriminator_kernel(tc, tensor, T_bytes, T_scale, out):
             t_scale = mxp.tile([P, PASSES, PACK], F32, name="t_scale")
             nc.scalar.dma_start(out=t_scale[:], in_=T_scale.rearrange("(g p t) a b -> p g (t a b)", p=P, t=PACK))
             bytes_view = T_bytes.rearrange("(g p t) j k -> g p (t j k)", p=P, t=PACK)
-            x_sb = mxp.tile([P, 2, IN_F], BF16, name="x_sb")
+            x_sb = keep.tile([P, 2, IN_F], BF16, name="x_sb")
             t_bytes = []
             for g in range(PASSES):
                 tb = bytes_pool.tile([P, PACK * IN_F], U8, name="t_bytes%d" % g)
@@ -102,7 +102,7 @@ def tile_minibatchdiscriminator_kernel(tc, tensor, T_bytes, T_scale, out):
                 if g == 0:
                     nc.sync.dma_start(out=x_sb[:], in_=tensor.rearrange("(h p) i -> p h i", p=P))
 
-            x_f32 = mxp.tile([P, 2, IN_F], F32, name="x_f32")
+            x_f32 = keep.tile([P, 2, IN_F], F32, name="x_f32")
             out_x = out[:, 0:IN_F].rearrange("(h p) i -> p h i", p=P)
             x_grouped = mxp.tile([P, PASSES, ROWS * PACK], BF16, name="x_grouped", align_bytes=64)
             x_codes = mxp.tile([P, PASSES * ROWS], U32, name="x_codes", align_bytes=64)

@@ -30,12 +30,16 @@ BATCH = 32
 VECTOR_ROWS = 128
 GPSIMD_ROWS = 24
 SCALAR_JOB = 4
+EXP_LAG = 1
+SCALAR_CASTS_EARLY = 0
+SCALAR_CASTS = 0
+LAST_WIDTHS = [2, 2, 2, 1, 1]
 BIG = 3.0e38
 PLANE = EXT + GROUP
 SLANTED = GPSIMD_ROWS + GROUP + P
 HALF = IN_F // 2
-VECTOR_CLOSING = 3
-VECTOR_BANKS = [3, 6]
+VECTOR_CLOSING = 2
+VECTOR_BANKS = []
 VECTOR_COLS = 384
 
 
@@ -188,6 +192,9 @@ def tile_minibatchdiscriminator_kernel(tc, tensor, T_bytes, T_scale, out):
                     quantize(PASSES - 1, half)
                     multiply(PASSES - 1, half)
                 closing = [(h, cb) for cb in (2, 3, 0, 1) for h in range(2)]
+                for h in range(SCALAR_CASTS_EARLY):
+                    nc.scalar.copy(out=x_f32[:, h, :], in_=x_sb[:, h, :])
+                    nc.sync.dma_start(out=out_x[:, h, :], in_=x_f32[:, h, :])
                 for i, (h, cb) in enumerate(closing):
                     dst = f_t[:, h, :, cb * 32:(cb + 1) * 32]
                     src = ft_bank[(h, cb)][:].rearrange("p (j k) -> p k j", k=KK)
@@ -212,8 +219,9 @@ def tile_minibatchdiscriminator_kernel(tc, tensor, T_bytes, T_scale, out):
                     for s in range(2):
                         for h in range(2):
                             nc.tensor.transpose(bank[:, s, h * P:(h + 1) * P], f_t[:, h, 2 * q + s, :], ident[:])
+                    if q in (3, 6):
+                        halve((3, 6).index(q), KK // 2)
                     if q in VECTOR_BANKS:
-                        halve(VECTOR_BANKS.index(q), KK // 2)
                         nc.vector.tensor_copy(out=f_ext[:, 2 * q:2 * q + 2, 0:ROWS], in_=bank[:])
                     else:
                         nc.scalar.copy(out=f_ext[:, 2 * q:2 * q + 2, 0:ROWS], in_=bank[:])
@@ -226,8 +234,11 @@ def tile_minibatchdiscriminator_kernel(tc, tensor, T_bytes, T_scale, out):
                 s_bank = psum.tile([P, ROWS], F32, name="s_bank", tag="bank7")
                 for h in range(2):
                     nc.tensor.transpose(s_bank[:, h * P:(h + 1) * P], s_t[:, h, :], ident[:])
-                for h in range(2):
-                    nc.vector.tensor_copy(out=x_f32[:, h, :], in_=x_sb[:, h, :])
+                for h in range(SCALAR_CASTS_EARLY, 2):
+                    if h < SCALAR_CASTS:
+                        nc.scalar.copy(out=x_f32[:, h, :], in_=x_sb[:, h, :])
+                    else:
+                        nc.vector.tensor_copy(out=x_f32[:, h, :], in_=x_sb[:, h, :])
                     nc.sync.dma_start(out=out_x[:, h, :], in_=x_f32[:, h, :])
                 nc.vector.tensor_copy(out=s_sum[:], in_=s_bank[:])
                 nc.vector.tensor_scalar(out=minus_half_s[:, 0:ROWS], in0=s_sum[:], scalar1=-0.5, scalar2=None, op0=ALU.mult)
@@ -247,9 +258,14 @@ def tile_minibatchdiscriminator_kernel(tc, tensor, T_bytes, T_scale, out):
         batches = [vector_groups[i:i + per_batch] for i in range(0, len(vector_groups), per_batch)]
         visits = [(b, q) for b in range(len(batches)) for q in range(PAIRS)]
         pieces_of = []
-        for number, (b, q) in enumerate(visits):
+        last_half = len(visits) - RING
+        for number, (b, q) in enumerate(visits[0:last_half]):
             width = 2 if q == PAIRS - 1 else len(batches[b])
             pieces_of.extend([(number, g0, min(g0 + width, len(batches[b]))) for g0 in range(0, len(batches[b]), width)])
+        g0 = 0
+        for width in LAST_WIDTHS:
+            pieces_of.extend([(number, g0, g0 + width) for number in range(last_half, len(visits))])
+            g0 += width
         vector_total = float(sum([g1 - g0 for number, g0, g1 in pieces_of]))
         gpsimd_pieces = []
         for m0 in range(VECTOR_ROWS, VECTOR_ROWS + GPSIMD_ROWS, GROUP):
@@ -309,12 +325,12 @@ def tile_minibatchdiscriminator_kernel(tc, tensor, T_bytes, T_scale, out):
                     fresh[0].append((acc[:, gi * GROUP:(gi + 1) * GROUP, :], batches[b][gi]))
 
         def release(route):
-            exps_due.extend(fresh[route])
+            exps_due.extend([(sums, m0, i_s) for sums, m0 in fresh[route]])
             fresh[route].clear()
 
         def group_exp(step):
-            if exps_due:
-                sums, m0 = exps_due.pop(0)
+            if exps_due and (exps_due[0][2] + EXP_LAG <= i_s or i_s >= len(scalar_rows) - 1):
+                sums, m0, since = exps_due.pop(0)
                 e = exp_pool.tile([P, GROUP, P + GROUP], F32, name="e", tag="e")
                 lead = own_pair(m0) * (GROUP - 1)
                 for r in range(sums.shape[1]):

@@ -44,13 +44,13 @@ VECTOR_COLS = 384
 
 
 def first_column(m):
+    return m + 1
+
+
+def window(m):
     if m < P:
-        return m + 1
-    return m
-
-
-def own_pair(m):
-    return m + 1 - first_column(m)
+        return P - 1
+    return P
 
 
 def tile_minibatchdiscriminator_kernel(tc, tensor, T_bytes, T_scale, out):
@@ -69,11 +69,9 @@ def tile_minibatchdiscriminator_kernel(tc, tensor, T_bytes, T_scale, out):
         nc.gpsimd.memset(zeros[:], 0.0)
         ones = keep.tile([P, 1], F32, name="ones")
         nc.gpsimd.memset(ones[:], 1.0)
-        not_first = keep.tile([P, 1], F32, name="not_first")
-        nc.vector.tensor_scalar(out=not_first[:], in0=ident[:, 0:1], scalar1=-1.0, scalar2=1.0, op0=ALU.mult, op1=ALU.add)
         col_sums = keep.tile([P, GROUP, PLANE], F32, name="col_sums")
         nc.gpsimd.memset(col_sums[:], 0.0)
-        nc.gpsimd.memset(col_sums[:, 0, GROUP - 1:GROUP - 1 + P], 1.0)
+        nc.gpsimd.memset(col_sums[:, 0, GROUP - 1:GROUP - 1 + ROWS], 1.0)
         row_sums = keep.tile([P, ROWS], F32, name="row_sums")
         totals_sb = keep.tile([P, EXT], F32, name="totals_sb")
         nc.gpsimd.memset(totals_sb[:], 0.0)
@@ -312,17 +310,18 @@ def tile_minibatchdiscriminator_kernel(tc, tensor, T_bytes, T_scale, out):
                         row = gi * GROUP + r
                         m = batches[b][gi] + r
                         c = first_column(m)
+                        w = window(m)
                         nc.vector.scalar_tensor_tensor(
-                            out=acc[:, row, :],
-                            in0=ring[v][:, s, c:c + P],
+                            out=acc[:, row, 0:w],
+                            in0=ring[v][:, s, c:c + w],
                             scalar=f_ext[:, k, m:m + 1],
-                            in1=(minus_half_s[:, c:c + P] if k == 0 else acc[:, row, :]),
+                            in1=(minus_half_s[:, c:c + w] if k == 0 else acc[:, row, 0:w]),
                             op0=ALU.max,
                             op1=ALU.add,
                         )
             if q == PAIRS - 1:
                 for gi in range(g0, g1):
-                    fresh[0].append((acc[:, gi * GROUP:(gi + 1) * GROUP, :], batches[b][gi]))
+                    fresh[0].append((acc[:, gi * GROUP:(gi + 1) * GROUP, 0:window(batches[b][gi])], batches[b][gi]))
 
         def release(route):
             exps_due.extend([(sums, m0, i_s) for sums, m0 in fresh[route]])
@@ -331,20 +330,18 @@ def tile_minibatchdiscriminator_kernel(tc, tensor, T_bytes, T_scale, out):
         def group_exp(step):
             if exps_due and (exps_due[0][2] + EXP_LAG <= i_s or i_s >= len(scalar_rows) - 1):
                 sums, m0, since = exps_due.pop(0)
-                e = exp_pool.tile([P, GROUP, P + GROUP], F32, name="e", tag="e")
-                lead = own_pair(m0) * (GROUP - 1)
+                e = exp_pool.tile([P, GROUP, P], F32, name="e", tag="e")
                 for r in range(sums.shape[1]):
                     m = m0 + r
-                    nc.scalar.activation(out=e[:, r, lead:lead + P], in_=sums[:, r, :], func=ACT.Exp, bias=s_sum[:, m:m + 1], scale=-2.0,
+                    nc.scalar.activation(out=e[:, r, 0:window(m)], in_=sums[:, r, :], func=ACT.Exp, bias=s_sum[:, m:m + 1], scale=-2.0,
                                          accum_out=row_sums[:, m:m + 1])
-                cols_due.append((e[:, 0:sums.shape[1], :], m0, step))
+                cols_due.append((e[:, 0:sums.shape[1], 0:window(m0)], m0, step))
 
         def add_columns(before):
             while cols_due and cols_due[0][2] < before:
                 e, m0, issued = cols_due.pop(0)
-                skip = own_pair(m0)
-                target = col_sums[:, 0:e.shape[1], m0 + GROUP:m0 + GROUP + P - skip]
-                nc.gpsimd.tensor_tensor(out=target, in0=target, in1=e[:, :, GROUP * skip:GROUP * skip + P - skip], op=ALU.add)
+                target = col_sums[:, 0:e.shape[1], m0 + GROUP:m0 + GROUP + e.shape[2]]
+                nc.gpsimd.tensor_tensor(out=target, in0=target, in1=e, op=ALU.add)
 
         def scalar_terms(m):
             terms = term_pool.tile([P, KK, P], F32, name="abs_terms", tag="abs_terms")
@@ -400,7 +397,7 @@ def tile_minibatchdiscriminator_kernel(tc, tensor, T_bytes, T_scale, out):
                                  is_transpose=True)
                 rows_left[0] -= 1
                 i = row_slot + m - scalar_first
-                nc.tensor.matmul(out=totals[:, i:i + 1], lhsT=turned[:, slot, :], rhs=(ones[:] if m < P else not_first[:]),
+                nc.tensor.matmul(out=totals[:, i:i + 1], lhsT=turned[:, slot, :], rhs=ones[:],
                                  start=False, stop=(rows_left[0] == 0))
 
         def finish_ready(before):

@@ -38,8 +38,8 @@ BIG = 3.0e38
 PLANE = EXT + GROUP
 SLANTED = GPSIMD_ROWS + GROUP + P
 HALF = IN_F // 2
-VECTOR_CLOSING = 2
-VECTOR_BANKS = []
+VECTOR_CLOSING = 3
+VECTOR_BANKS = [1, 3, 5, 7]
 VECTOR_COLS = 384
 
 
@@ -73,6 +73,7 @@ def tile_minibatchdiscriminator_kernel(tc, tensor, T_bytes, T_scale, out):
         nc.gpsimd.memset(col_sums[:], 0.0)
         nc.gpsimd.memset(col_sums[:, 0, GROUP - 1:GROUP - 1 + ROWS], 1.0)
         row_sums = keep.tile([P, ROWS], F32, name="row_sums")
+        nc.gpsimd.memset(row_sums[:], 0.0)
         totals_sb = keep.tile([P, EXT], F32, name="totals_sb")
         nc.gpsimd.memset(totals_sb[:], 0.0)
 
@@ -217,8 +218,6 @@ def tile_minibatchdiscriminator_kernel(tc, tensor, T_bytes, T_scale, out):
                     for s in range(2):
                         for h in range(2):
                             nc.tensor.transpose(bank[:, s, h * P:(h + 1) * P], f_t[:, h, 2 * q + s, :], ident[:])
-                    if q in (3, 6):
-                        halve((3, 6).index(q), KK // 2)
                     if q in VECTOR_BANKS:
                         nc.vector.tensor_copy(out=f_ext[:, 2 * q:2 * q + 2, 0:ROWS], in_=bank[:])
                     else:
@@ -226,7 +225,7 @@ def tile_minibatchdiscriminator_kernel(tc, tensor, T_bytes, T_scale, out):
                     if q % 2 == 1:
                         nc.gpsimd.tensor_scalar(out=f_ext[:, 2 * q - 2:2 * q + 2, ROWS:EXT], in0=f_ext[:, 2 * q - 2:2 * q + 2, 0:P], scalar1=1.0,
                                                 scalar2=0.0, op0=ALU.mult, op1=ALU.add)
-                for half in (4, 2, 1):
+                for half in (8, 4, 2, 1):
                     for h in range(2):
                         halve(h, half)
                 s_bank = psum.tile([P, ROWS], F32, name="s_bank", tag="bank7")
@@ -396,7 +395,7 @@ def tile_minibatchdiscriminator_kernel(tc, tensor, T_bytes, T_scale, out):
                 nc.tensor.matmul(out=totals[:, c:c + P], lhsT=turned[:, slot, :], rhs=ident[:], start=False, stop=False,
                                  is_transpose=True)
                 rows_left[0] -= 1
-                i = row_slot + m - scalar_first
+                i = m - scalar_first
                 nc.tensor.matmul(out=totals[:, i:i + 1], lhsT=turned[:, slot, :], rhs=ones[:],
                                  start=False, stop=(rows_left[0] == 0))
 
@@ -442,7 +441,7 @@ def tile_minibatchdiscriminator_kernel(tc, tensor, T_bytes, T_scale, out):
                     add_terms(open_job[0], m, pieces)
                     group_exp(step)
                     finish_ready(i_s - 1)
-                    if len(open_job[0][0]) == SCALAR_JOB or i_s == len(scalar_rows) - 1:
+                    if len(open_job[0][0]) == SCALAR_JOB or i_s >= len(scalar_rows) - 3:
                         ready.append((open_job.pop(0), i_s))
                     i_s += 1
                 else:
@@ -468,20 +467,22 @@ def tile_minibatchdiscriminator_kernel(tc, tensor, T_bytes, T_scale, out):
             finish_ready(i_s)
             add_columns(step + 1)
 
-        nc.scalar.copy(out=totals_sb[:, scalar_first:EXT], in_=totals[:, 0:row_slot])
-        nc.vector.tensor_copy(out=row_sums[:, scalar_first:ROWS], in_=totals[:, row_slot:row_slot + ROWS - scalar_first])
+        nc.scalar.copy(out=totals_sb[:, ROWS:EXT], in_=totals[:, ROWS - scalar_first:EXT - scalar_first])
+        nc.vector.tensor_copy(out=totals_sb[:, scalar_first:ROWS], in_=totals[:, 0:ROWS - scalar_first])
 
-        diversity = psum.tile([P, 2, P], F32, name="diversity", tag="bank0")
+        diversity = []
         for h in range(2):
-            block = slice(h * P, (h + 1) * P)
-            parts = [row_sums[:, block], totals_sb[:, block]]
+            half_sum = psum.tile([P, P], F32, name="diversity%d" % h, tag="bank%d" % h)
+            diversity.append(half_sum)
+            parts = [row_sums[:, h * P:(h + 1) * P]]
             if h == 0:
-                parts.append(totals_sb[:, ROWS:EXT])
                 parts.extend([col_sums[:, r, GROUP - 1 - r + ROWS:GROUP - 1 - r + EXT] for r in range(GROUP)])
             parts.extend([col_sums[:, r, GROUP - 1 - r + h * P:GROUP - 1 - r + (h + 1) * P] for r in range(GROUP)])
             for i, part in enumerate(parts):
-                nc.tensor.matmul(out=diversity[:, h, :], lhsT=part, rhs=ident[:], start=(i == 0), stop=(i == len(parts) - 1),
-                                 is_transpose=True)
+                nc.tensor.matmul(out=half_sum[:], lhsT=part, rhs=ident[:], start=(i == 0), stop=False, is_transpose=True)
         diversity_sb = keep.tile([P, 2, P], F32, name="diversity_sb")
-        nc.vector.tensor_copy(out=diversity_sb[:], in_=diversity[:])
+        nc.tensor.matmul(out=diversity[0][:], lhsT=totals_sb[:, ROWS:EXT], rhs=ident[:], start=False, stop=True, is_transpose=True)
+        nc.scalar.copy(out=diversity_sb[:, 0, :], in_=diversity[0][:])
+        nc.tensor.matmul(out=diversity[1][:], lhsT=totals_sb[:, P:ROWS], rhs=ident[:], start=False, stop=True, is_transpose=True)
+        nc.vector.tensor_copy(out=diversity_sb[:, 1, :], in_=diversity[1][:])
         nc.sync.dma_start(out=out[:, IN_F:IN_F + P].rearrange("(h p) j -> p h j", p=P), in_=diversity_sb[:])

@@ -253,11 +253,13 @@ def tile_minibatchdiscriminator_kernel(tc, tensor, T_bytes, T_scale, out):
         vector_groups = list(range(0, VECTOR_ROWS, GROUP))
         per_batch = BATCH // GROUP
         batches = [vector_groups[i:i + per_batch] for i in range(0, len(vector_groups), per_batch)]
-        visits = [(b, q) for b in range(len(batches)) for q in range(PAIRS)]
+        visits = []
+        for b in range(len(batches)):
+            visits.extend([(b, q if b % 2 == 0 else PAIRS - 1 - q) for q in range(PAIRS)])
         pieces_of = []
         last_half = len(visits) - RING
         for number, (b, q) in enumerate(visits[0:last_half]):
-            width = 2 if q == PAIRS - 1 else len(batches[b])
+            width = 2 if number % PAIRS == PAIRS - 1 else len(batches[b])
             pieces_of.extend([(number, g0, min(g0 + width, len(batches[b]))) for g0 in range(0, len(batches[b]), width)])
         g0 = 0
         for width in LAST_WIDTHS:
@@ -289,8 +291,12 @@ def tile_minibatchdiscriminator_kernel(tc, tensor, T_bytes, T_scale, out):
         own_terms = []
 
         def refill(v):
-            q = visits[v][1]
-            bank = psum.tile([P, 2, ROWS], F32, name="ring", tag="bank%d" % (v % RING))
+            b, q = visits[v]
+            place = v % PAIRS
+            if place < RING:
+                ring[v] = ring[v - 1 - 2 * place]
+                return
+            bank = psum.tile([P, 2, ROWS], F32, name="ring", tag="bank%d" % (place % RING if b % 2 == 0 else RING - 1 - place % RING))
             for s in range(2):
                 for h in range(2):
                     nc.tensor.transpose(bank[:, s, h * P:(h + 1) * P], f_t[:, h, 2 * q + s, :], ident[:])
@@ -298,7 +304,7 @@ def tile_minibatchdiscriminator_kernel(tc, tensor, T_bytes, T_scale, out):
 
         def vector_visit(v, g0, g1):
             b, q = visits[v]
-            if q == 0:
+            if v % PAIRS == 0:
                 acc_new = acc_pool.tile([P, BATCH, P], F32, name="acc", tag="acc")
                 acc_of[b] = acc_new
             acc = acc_of[b]
@@ -314,11 +320,11 @@ def tile_minibatchdiscriminator_kernel(tc, tensor, T_bytes, T_scale, out):
                             out=acc[:, row, 0:w],
                             in0=ring[v][:, s, c:c + w],
                             scalar=f_ext[:, k, m:m + 1],
-                            in1=(minus_half_s[:, c:c + w] if k == 0 else acc[:, row, 0:w]),
+                            in1=(minus_half_s[:, c:c + w] if v % PAIRS == 0 and s == 0 else acc[:, row, 0:w]),
                             op0=ALU.max,
                             op1=ALU.add,
                         )
-            if q == PAIRS - 1:
+            if v % PAIRS == PAIRS - 1:
                 for gi in range(g0, g1):
                     fresh[0].append((acc[:, gi * GROUP:(gi + 1) * GROUP, 0:window(batches[b][gi])], batches[b][gi]))
 

@@ -30,7 +30,10 @@ BATCH = 32
 VECTOR_ROWS = 128
 GPSIMD_ROWS = 24
 SCALAR_JOB = 4
-EXP_LAG = 1
+EXP_LAG = 2
+JOB_LAG = 3
+TERM_BUFS = 6
+EXP_BUFS = 8
 SCALAR_CASTS_EARLY = 0
 SCALAR_CASTS = 0
 LAST_WIDTHS = [2, 2, 2, 1, 1]
@@ -245,8 +248,8 @@ def tile_minibatchdiscriminator_kernel(tc, tensor, T_bytes, T_scale, out):
 
 
         acc_pool = ctx.enter_context(tc.tile_pool(name="acc_pool", bufs=2))
-        exp_pool = ctx.enter_context(tc.tile_pool(name="exp_pool", bufs=8))
-        term_pool = ctx.enter_context(tc.tile_pool(name="term_pool", bufs=4))
+        exp_pool = ctx.enter_context(tc.tile_pool(name="exp_pool", bufs=EXP_BUFS))
+        term_pool = ctx.enter_context(tc.tile_pool(name="term_pool", bufs=TERM_BUFS))
         own_pool = ctx.enter_context(tc.tile_pool(name="own_pool", bufs=2))
         turned_pool = ctx.enter_context(tc.tile_pool(name="turned_pool", bufs=3))
 
@@ -446,7 +449,7 @@ def tile_minibatchdiscriminator_kernel(tc, tensor, T_bytes, T_scale, out):
                         open_job.append(new_job())
                     add_terms(open_job[0], m, pieces)
                     group_exp(step)
-                    finish_ready(i_s - 1)
+                    finish_ready(i_s + 1 - JOB_LAG)
                     if len(open_job[0][0]) == SCALAR_JOB or i_s >= len(scalar_rows) - 3:
                         ready.append((open_job.pop(0), i_s))
                     i_s += 1

@@ -34,15 +34,14 @@ EXP_LAG = 2
 JOB_LAG = 3
 TERM_BUFS = 6
 EXP_BUFS = 8
-SCALAR_CASTS_EARLY = 0
-SCALAR_CASTS = 0
 LAST_WIDTHS = [2, 2, 2, 1, 1]
 BIG = 3.0e38
 PLANE = EXT + GROUP
 SLANTED = GPSIMD_ROWS + GROUP + P
 HALF = IN_F // 2
 VECTOR_CLOSING = 3
-VECTOR_BANKS = [1, 3, 5, 7]
+SCALAR_BANKS = [0, 1]
+X_ON_VECTOR = []
 VECTOR_COLS = 384
 
 
@@ -80,13 +79,19 @@ def tile_minibatchdiscriminator_kernel(tc, tensor, T_bytes, T_scale, out):
         totals_sb = keep.tile([P, EXT], F32, name="totals_sb")
         nc.gpsimd.memset(totals_sb[:], 0.0)
 
-        f_ext = keep.tile([P, KK, EXT], F32, name="f_ext")
+        f_sw = keep.tile([P, KK, ROWS], F32, name="f_sw")
         f_t = keep.tile([P, 2, KK, P], F32, name="f_t")
-        s_t = keep.tile([P, 2, P], F32, name="s_t")
         s_sum = keep.tile([P, ROWS], F32, name="s_sum")
         minus_half_s = keep.tile([P, EXT], F32, name="minus_half_s")
         minus_half_s_slanted = keep.tile([P, GROUP, SLANTED], F32, name="minus_half_s_slanted")
         f_bank = []
+
+        def f_columns(k, c):
+            return f_sw[:, k, c - P:c]
+
+        def f_value(k, m):
+            place = (m + P) % ROWS
+            return f_sw[:, k, place:place + 1]
 
         with ExitStack() as head:
             bytes_pool = head.enter_context(tc.tile_pool(name="bytes_pool", bufs=1))
@@ -104,9 +109,10 @@ def tile_minibatchdiscriminator_kernel(tc, tensor, T_bytes, T_scale, out):
                 for piece in range(pieces):
                     run = slice(piece * PACK * IN_F // pieces, (piece + 1) * PACK * IN_F // pieces)
                     nc.sync.dma_start(out=tb[:, run], in_=bytes_view[g][:, run])
+                    if g == 0:
+                        x_cols = slice(piece * P * PACK, (piece + 1) * P * PACK)
+                        nc.sync.dma_start(out=x_sb[:, :, x_cols], in_=tensor.rearrange("(h p) i -> p h i", p=P)[:, :, x_cols])
                 t_bytes.append(tb)
-                if g == 0:
-                    nc.sync.dma_start(out=x_sb[:], in_=tensor.rearrange("(h p) i -> p h i", p=P))
 
             x_f32 = keep.tile([P, 2, IN_F], F32, name="x_f32")
             out_x = out[:, 0:IN_F].rearrange("(h p) i -> p h i", p=P)
@@ -162,10 +168,11 @@ def tile_minibatchdiscriminator_kernel(tc, tensor, T_bytes, T_scale, out):
                         words = x_sb[:, h, :].bitcast(F32)
                         for u in range(2):
                             nc.tensor.transpose(x_t[:, h, u, :], words[:, 256 * g + u:256 * (g + 1):2], ident[:])
-                    nc.vector.tensor_copy(
-                        out=x_grouped[:, g, :].bitcast(F32).rearrange("p (h r u) -> p h r u", h=2, u=2),
-                        in_=x_t[:].rearrange("p h u r -> p h r u"),
-                    )
+                    x_dst = x_grouped[:, g, :].bitcast(F32).rearrange("p (h r u) -> p h r u", h=2, u=2)
+                    if g in X_ON_VECTOR:
+                        nc.vector.tensor_copy(out=x_dst, in_=x_t[:].rearrange("p h u r -> p h r u"))
+                    else:
+                        nc.scalar.copy(out=x_dst, in_=x_t[:].rearrange("p h u r -> p h r u"))
                 for h in range(2):
                     for cb in range(4):
                         bank = psum.tile([P, 512], F32, name="ft_bank%d" % (4 * h + cb), tag="bank%d" % (4 * h + cb))
@@ -194,9 +201,6 @@ def tile_minibatchdiscriminator_kernel(tc, tensor, T_bytes, T_scale, out):
                     quantize(PASSES - 1, half)
                     multiply(PASSES - 1, half)
                 closing = [(h, cb) for cb in (2, 3, 0, 1) for h in range(2)]
-                for h in range(SCALAR_CASTS_EARLY):
-                    nc.scalar.copy(out=x_f32[:, h, :], in_=x_sb[:, h, :])
-                    nc.sync.dma_start(out=out_x[:, h, :], in_=x_f32[:, h, :])
                 for i, (h, cb) in enumerate(closing):
                     dst = f_t[:, h, :, cb * 32:(cb + 1) * 32]
                     src = ft_bank[(h, cb)][:].rearrange("p (j k) -> p k j", k=KK)
@@ -205,40 +209,29 @@ def tile_minibatchdiscriminator_kernel(tc, tensor, T_bytes, T_scale, out):
                     else:
                         nc.vector.tensor_copy(out=dst, in_=src)
 
-                tree = stage.tile([P, 2, KK // 2, P], F32, name="tree", tag="w")
-
-                def halve(h, half):
-                    if half == KK // 2:
-                        nc.vector.tensor_tensor(out=tree[:, h, :, :], in0=f_t[:, h, 0:half, :], in1=f_t[:, h, half:2 * half, :], op=ALU.add)
-                    elif half > 1:
-                        nc.vector.tensor_tensor(out=tree[:, h, 0:half, :], in0=tree[:, h, 0:half, :], in1=tree[:, h, half:2 * half, :], op=ALU.add)
-                    else:
-                        nc.vector.tensor_tensor(out=s_t[:, h, :], in0=tree[:, h, 0, :], in1=tree[:, h, 1, :], op=ALU.add)
-
                 for q in range(PAIRS):
                     bank = psum.tile([P, 2, ROWS], F32, name="f_bank%d" % q, tag="bank%d" % q)
                     f_bank.append(bank)
                     for s in range(2):
                         for h in range(2):
-                            nc.tensor.transpose(bank[:, s, h * P:(h + 1) * P], f_t[:, h, 2 * q + s, :], ident[:])
-                    if q in VECTOR_BANKS:
-                        nc.vector.tensor_copy(out=f_ext[:, 2 * q:2 * q + 2, 0:ROWS], in_=bank[:])
+                            half = h if q < RING else 1 - h
+                            nc.tensor.transpose(bank[:, s, half * P:(half + 1) * P], f_t[:, h, 2 * q + s, :], ident[:])
+                    if q < RING:
+                        moves = [(f_sw[:, 2 * q:2 * q + 2, P:ROWS], bank[:, :, 0:P]), (f_sw[:, 2 * q:2 * q + 2, 0:P], bank[:, :, P:ROWS])]
                     else:
-                        nc.scalar.copy(out=f_ext[:, 2 * q:2 * q + 2, 0:ROWS], in_=bank[:])
-                    if q % 2 == 1:
-                        nc.gpsimd.tensor_scalar(out=f_ext[:, 2 * q - 2:2 * q + 2, ROWS:EXT], in0=f_ext[:, 2 * q - 2:2 * q + 2, 0:P], scalar1=1.0,
-                                                scalar2=0.0, op0=ALU.mult, op1=ALU.add)
-                for half in (8, 4, 2, 1):
-                    for h in range(2):
-                        halve(h, half)
-                s_bank = psum.tile([P, ROWS], F32, name="s_bank", tag="bank7")
+                        moves = [(f_sw[:, 2 * q:2 * q + 2, :], bank[:])]
+                    for dst, part in moves:
+                        if q in SCALAR_BANKS:
+                            nc.scalar.copy(out=dst, in_=part)
+                        else:
+                            nc.vector.tensor_copy(out=dst, in_=part)
+                s_bank = psum.tile([P, ROWS], F32, name="s_bank", tag="bank%d" % RING)
                 for h in range(2):
-                    nc.tensor.transpose(s_bank[:, h * P:(h + 1) * P], s_t[:, h, :], ident[:])
-                for h in range(SCALAR_CASTS_EARLY, 2):
-                    if h < SCALAR_CASTS:
-                        nc.scalar.copy(out=x_f32[:, h, :], in_=x_sb[:, h, :])
-                    else:
-                        nc.vector.tensor_copy(out=x_f32[:, h, :], in_=x_sb[:, h, :])
+                    for k in range(KK):
+                        nc.tensor.matmul(out=s_bank[:, h * P:(h + 1) * P], lhsT=f_t[:, h, k, :], rhs=ident[:], start=(k == 0), stop=(k == KK - 1),
+                                         is_transpose=True)
+                for h in range(2):
+                    nc.vector.tensor_copy(out=x_f32[:, h, :], in_=x_sb[:, h, :])
                     nc.sync.dma_start(out=out_x[:, h, :], in_=x_f32[:, h, :])
                 nc.vector.tensor_copy(out=s_sum[:], in_=s_bank[:])
                 nc.vector.tensor_scalar(out=minus_half_s[:, 0:ROWS], in0=s_sum[:], scalar1=-0.5, scalar2=None, op0=ALU.mult)
@@ -322,7 +315,7 @@ def tile_minibatchdiscriminator_kernel(tc, tensor, T_bytes, T_scale, out):
                         nc.vector.scalar_tensor_tensor(
                             out=acc[:, row, 0:w],
                             in0=ring[v][:, s, c:c + w],
-                            scalar=f_ext[:, k, m:m + 1],
+                            scalar=f_value(k, m),
                             in1=(minus_half_s[:, c:c + w] if v % PAIRS == 0 and s == 0 else acc[:, row, 0:w]),
                             op0=ALU.max,
                             op1=ALU.add,
@@ -355,7 +348,7 @@ def tile_minibatchdiscriminator_kernel(tc, tensor, T_bytes, T_scale, out):
             terms = term_pool.tile([P, KK, P], F32, name="abs_terms", tag="abs_terms")
             c = first_column(m)
             for k in range(KK):
-                nc.scalar.activation(out=terms[:, k, :], in_=f_ext[:, k, c:c + P], func=ACT.Abs, bias=f_ext[:, k, m:m + 1],
+                nc.scalar.activation(out=terms[:, k, :], in_=f_columns(k, c), func=ACT.Abs, bias=f_value(k, m),
                                      scale=-1.0)
             return [terms[:, k, :] for k in range(KK)]
 
@@ -367,8 +360,8 @@ def tile_minibatchdiscriminator_kernel(tc, tensor, T_bytes, T_scale, out):
                 own_terms.append(terms_new)
             c = first_column(m)
             for k in range(KK):
-                nc.gpsimd.tensor_scalar(out=own_terms[0][:, r, k, :], in0=f_ext[:, k, c:c + P], scalar1=BIG,
-                                        scalar2=f_ext[:, k, m:m + 1], op0=ALU.min, op1=ALU.max)
+                nc.gpsimd.tensor_scalar(out=own_terms[0][:, r, k, :], in0=f_columns(k, c), scalar1=BIG,
+                                        scalar2=f_value(k, m), op0=ALU.min, op1=ALU.max)
 
         def gpsimd_halve(n, half):
             terms = own_terms[0]
@@ -383,7 +376,7 @@ def tile_minibatchdiscriminator_kernel(tc, tensor, T_bytes, T_scale, out):
             fresh[2].append((sums[:, 0:n, :], m0))
 
         def new_job():
-            bank = psum.tile([P, SCALAR_JOB, P], F32, name="job", tag="bank%d" % (RING + len(jobs) % JOB_BANKS))
+            bank = psum.tile([P, SCALAR_JOB, P], F32, name="job", tag="bank%d" % (RING + (len(jobs) + 1) % JOB_BANKS))
             job = [[], bank]
             jobs.append(job)
             return job

@@ -342,7 +342,10 @@ def tile_minibatchdiscriminator_kernel(tc, tensor, T_bytes, T_scale, out):
             while cols_due and cols_due[0][2] < before:
                 e, m0, issued = cols_due.pop(0)
                 target = col_sums[:, 0:e.shape[1], m0 + GROUP:m0 + GROUP + e.shape[2]]
-                nc.gpsimd.tensor_tensor(out=target, in0=target, in1=e, op=ALU.add)
+                if m0 == VECTOR_ROWS - GROUP:
+                    nc.vector.tensor_tensor(out=target, in0=target, in1=e, op=ALU.add)
+                else:
+                    nc.gpsimd.tensor_tensor(out=target, in0=target, in1=e, op=ALU.add)
 
         def scalar_terms(m):
             terms = term_pool.tile([P, KK, P], F32, name="abs_terms", tag="abs_terms")
@@ -457,13 +460,15 @@ def tile_minibatchdiscriminator_kernel(tc, tensor, T_bytes, T_scale, out):
                         gpsimd_last(first, second)
                     gpsimd_done += elements
                     i_g += 1
+                if i_g == len(gpsimd_pieces):
+                    release(2)
                 if i_s == len(scalar_rows):
                     group_exp(step)
                     finish_ready(i_s)
                 add_columns(step - 1)
             step += 1
-            release(0)
             release(2)
+            release(0)
             while exps_due:
                 group_exp(step)
             finish_ready(i_s)
@@ -476,12 +481,15 @@ def tile_minibatchdiscriminator_kernel(tc, tensor, T_bytes, T_scale, out):
         for h in range(2):
             half_sum = psum.tile([P, P], F32, name="diversity%d" % h, tag="bank%d" % h)
             diversity.append(half_sum)
-            parts = [row_sums[:, h * P:(h + 1) * P]]
-            if h == 0:
-                parts.extend([col_sums[:, r, GROUP - 1 - r + ROWS:GROUP - 1 - r + EXT] for r in range(GROUP)])
-            parts.extend([col_sums[:, r, GROUP - 1 - r + h * P:GROUP - 1 - r + (h + 1) * P] for r in range(GROUP)])
-            for i, part in enumerate(parts):
-                nc.tensor.matmul(out=half_sum[:], lhsT=part, rhs=ident[:], start=(i == 0), stop=False, is_transpose=True)
+        parts = [(0, col_sums[:, r, GROUP - 1 - r + ROWS:GROUP - 1 - r + EXT]) for r in range(GROUP)]
+        parts.append((1, row_sums[:, P:ROWS]))
+        parts.append((0, row_sums[:, 0:P]))
+        for h in range(2):
+            parts.extend([(h, col_sums[:, r, GROUP - 1 - r + h * P:GROUP - 1 - r + (h + 1) * P]) for r in range(GROUP)])
+        opened = set()
+        for h, part in parts:
+            nc.tensor.matmul(out=diversity[h][:], lhsT=part, rhs=ident[:], start=(h not in opened), stop=False, is_transpose=True)
+            opened.add(h)
         diversity_sb = keep.tile([P, 2, P], F32, name="diversity_sb")
         nc.tensor.matmul(out=diversity[0][:], lhsT=totals_sb[:, ROWS:EXT], rhs=ident[:], start=False, stop=True, is_transpose=True)
         nc.scalar.copy(out=diversity_sb[:, 0, :], in_=diversity[0][:])

@@ -28,6 +28,7 @@ JOB_BANKS = 3
 GROUP = 4
 BATCH = 32
 VECTOR_ROWS = 128
+FIRST_VECTOR_ROW = 1
 GPSIMD_ROWS = 24
 SCALAR_JOB = 4
 EXP_LAG = 2
@@ -46,6 +47,8 @@ VECTOR_COLS = 384
 
 
 def first_column(m):
+    if m == ROWS:
+        return m
     return m + 1
 
 
@@ -74,6 +77,7 @@ def tile_minibatchdiscriminator_kernel(tc, tensor, T_bytes, T_scale, out):
         col_sums = keep.tile([P, GROUP, PLANE], F32, name="col_sums")
         nc.gpsimd.memset(col_sums[:], 0.0)
         nc.gpsimd.memset(col_sums[:, 0, GROUP - 1:GROUP - 1 + ROWS], 1.0)
+        nc.gpsimd.memset(col_sums[:, 0, GROUP - 1:GROUP - 1 + FIRST_VECTOR_ROW], -1.0)
         row_sums = keep.tile([P, ROWS], F32, name="row_sums")
         nc.gpsimd.memset(row_sums[:], 0.0)
         totals_sb = keep.tile([P, EXT], F32, name="totals_sb")
@@ -270,7 +274,7 @@ def tile_minibatchdiscriminator_kernel(tc, tensor, T_bytes, T_scale, out):
             gpsimd_pieces.append(("last", m0, n, n * P))
         gpsimd_total = float(sum([piece[3] for piece in gpsimd_pieces]))
         scalar_first = VECTOR_ROWS + GPSIMD_ROWS
-        scalar_rows = list(range(scalar_first, ROWS))
+        scalar_rows = list(range(scalar_first, ROWS + FIRST_VECTOR_ROW))
         row_slot = EXT - scalar_first
         rows_left = [len(scalar_rows)]
 
@@ -310,6 +314,8 @@ def tile_minibatchdiscriminator_kernel(tc, tensor, T_bytes, T_scale, out):
                     for r in range(GROUP):
                         row = gi * GROUP + r
                         m = batches[b][gi] + r
+                        if m < FIRST_VECTOR_ROW:
+                            continue
                         c = first_column(m)
                         w = window(m)
                         nc.vector.scalar_tensor_tensor(
@@ -322,7 +328,8 @@ def tile_minibatchdiscriminator_kernel(tc, tensor, T_bytes, T_scale, out):
                         )
             if v % PAIRS == PAIRS - 1:
                 for gi in range(g0, g1):
-                    fresh[0].append((acc[:, gi * GROUP:(gi + 1) * GROUP, 0:window(batches[b][gi])], batches[b][gi]))
+                    first = max(batches[b][gi], FIRST_VECTOR_ROW)
+                    fresh[0].append((acc[:, gi * GROUP + first - batches[b][gi]:(gi + 1) * GROUP, 0:window(first)], first))
 
         def release(route):
             exps_due.extend([(sums, m0, i_s) for sums, m0 in fresh[route]])

@@ -321,7 +321,7 @@ def tile_minibatchdiscriminator_kernel(tc, tensor, T_bytes, T_scale, out):
                         nc.vector.scalar_tensor_tensor(
                             out=acc[:, row, 0:w],
                             in0=ring[v][:, s, c:c + w],
-                            scalar=f_value(k, m),
+                            scalar=ring[v][:, s, m:m + 1],
                             in1=(minus_half_s[:, c:c + w] if v % PAIRS == 0 and s == 0 else acc[:, row, 0:w]),
                             op0=ALU.max,
                             op1=ALU.add,

@@ -32,6 +32,8 @@ FIRST_VECTOR_ROW = 1
 GPSIMD_ROWS = 24
 SCALAR_JOB = 4
 EXP_LAG = 2
+LAST_ROWS = 12
+GPSIMD_AHEAD = 0.98
 JOB_LAG = 3
 TERM_BUFS = 6
 EXP_BUFS = 8
@@ -336,7 +338,8 @@ def tile_minibatchdiscriminator_kernel(tc, tensor, T_bytes, T_scale, out):
             fresh[route].clear()
 
         def group_exp(step):
-            if exps_due and (exps_due[0][2] + EXP_LAG <= i_s or i_s >= len(scalar_rows) - 1):
+            lag = EXP_LAG if i_s < len(scalar_rows) - LAST_ROWS else EXP_LAG - 1
+            if exps_due and (exps_due[0][2] + lag <= i_s or i_s >= len(scalar_rows) - 1):
                 sums, m0, since = exps_due.pop(0)
                 e = exp_pool.tile([P, GROUP, P], F32, name="e", tag="e")
                 for r in range(sums.shape[1]):
@@ -434,7 +437,7 @@ def tile_minibatchdiscriminator_kernel(tc, tensor, T_bytes, T_scale, out):
                 if i_s < len(scalar_rows):
                     shares.append((i_s / float(len(scalar_rows)), 1))
                 if i_g < len(gpsimd_pieces):
-                    shares.append((gpsimd_done / gpsimd_total, 2))
+                    shares.append((gpsimd_done / gpsimd_total * GPSIMD_AHEAD, 2))
                 route = min(shares)[1]
                 step += 1
                 if route == 0:

@@ -73,22 +73,22 @@ def tile_minibatchdiscriminator_kernel(tc, tensor, T_bytes, T_scale, out):
         ident = keep.tile([P, P], F32, name="ident")
         make_identity(nc, ident[:])
         zeros = keep.tile([P, P], F32, name="zeros")
-        nc.gpsimd.memset(zeros[:], 0.0)
+        nc.vector.memset(zeros[:], 0.0)
         ones = keep.tile([P, 1], F32, name="ones")
         nc.gpsimd.memset(ones[:], 1.0)
         col_sums = keep.tile([P, GROUP, PLANE], F32, name="col_sums")
-        nc.gpsimd.memset(col_sums[:], 0.0)
-        nc.gpsimd.memset(col_sums[:, 0, GROUP - 1:GROUP - 1 + ROWS], 1.0)
-        nc.gpsimd.memset(col_sums[:, 0, GROUP - 1:GROUP - 1 + FIRST_VECTOR_ROW], -1.0)
+        nc.vector.memset(col_sums[:], 0.0)
+        nc.vector.memset(col_sums[:, 0, GROUP - 1:GROUP - 1 + ROWS], 1.0)
+        nc.vector.memset(col_sums[:, 0, GROUP - 1:GROUP - 1 + FIRST_VECTOR_ROW], -1.0)
         row_sums = keep.tile([P, ROWS], F32, name="row_sums")
-        nc.gpsimd.memset(row_sums[:], 0.0)
+        nc.vector.memset(row_sums[:], 0.0)
         totals_sb = keep.tile([P, EXT], F32, name="totals_sb")
-        nc.gpsimd.memset(totals_sb[:], 0.0)
+        nc.vector.memset(totals_sb[:], 0.0)
 
         f_sw = keep.tile([P, KK, ROWS], F32, name="f_sw")
         f_t = keep.tile([P, 2, KK, P], F32, name="f_t")
         s_sum = keep.tile([P, ROWS], F32, name="s_sum")
-        minus_half_s = keep.tile([P, EXT], F32, name="minus_half_s")
+        minus_half_s = keep.tile([P, ROWS], F32, name="minus_half_s")
         minus_half_s_slanted = keep.tile([P, GROUP, SLANTED], F32, name="minus_half_s_slanted")
         f_bank = []
 
@@ -207,6 +207,12 @@ def tile_minibatchdiscriminator_kernel(tc, tensor, T_bytes, T_scale, out):
                     quantize(PASSES - 1, half)
                     multiply(PASSES - 1, half)
                 closing = [(h, cb) for cb in (2, 3, 0, 1) for h in range(2)]
+
+                def cast(h):
+                    nc.vector.tensor_copy(out=x_f32[:, h, :], in_=x_sb[:, h, :])
+                    nc.sync.dma_start(out=out_x[:, h, :], in_=x_f32[:, h, :])
+
+                cast(0)
                 for i, (h, cb) in enumerate(closing):
                     dst = f_t[:, h, :, cb * 32:(cb + 1) * 32]
                     src = ft_bank[(h, cb)][:].rearrange("p (j k) -> p k j", k=KK)
@@ -215,6 +221,7 @@ def tile_minibatchdiscriminator_kernel(tc, tensor, T_bytes, T_scale, out):
                     else:
                         nc.vector.tensor_copy(out=dst, in_=src)
 
+                cast(1)
                 for q in range(PAIRS):
                     bank = psum.tile([P, 2, ROWS], F32, name="f_bank%d" % q, tag="bank%d" % q)
                     f_bank.append(bank)
@@ -236,14 +243,14 @@ def tile_minibatchdiscriminator_kernel(tc, tensor, T_bytes, T_scale, out):
                     for k in range(KK):
                         nc.tensor.matmul(out=s_bank[:, h * P:(h + 1) * P], lhsT=f_t[:, h, k, :], rhs=ident[:], start=(k == 0), stop=(k == KK - 1),
                                          is_transpose=True)
-                for h in range(2):
-                    nc.vector.tensor_copy(out=x_f32[:, h, :], in_=x_sb[:, h, :])
-                    nc.sync.dma_start(out=out_x[:, h, :], in_=x_f32[:, h, :])
+                nc.vector.tensor_scalar(out=minus_half_s[:], in0=s_bank[:], scalar1=-0.5, scalar2=None, op0=ALU.mult)
                 nc.vector.tensor_copy(out=s_sum[:], in_=s_bank[:])
-                nc.vector.tensor_scalar(out=minus_half_s[:, 0:ROWS], in0=s_sum[:], scalar1=-0.5, scalar2=None, op0=ALU.mult)
-                nc.vector.tensor_scalar(out=minus_half_s[:, ROWS:EXT], in0=s_sum[:, 0:P], scalar1=-0.5, scalar2=None, op0=ALU.mult)
                 for r in range(GROUP):
-                    nc.vector.tensor_copy(out=minus_half_s_slanted[:, r, :], in_=minus_half_s[:, VECTOR_ROWS + r:VECTOR_ROWS + r + SLANTED])
+                    straight = ROWS - VECTOR_ROWS - r
+                    nc.vector.tensor_scalar(out=minus_half_s_slanted[:, r, 0:straight], in0=s_bank[:, VECTOR_ROWS + r:ROWS], scalar1=-0.5,
+                                            scalar2=None, op0=ALU.mult)
+                    nc.vector.tensor_scalar(out=minus_half_s_slanted[:, r, straight:SLANTED], in0=s_bank[:, 0:SLANTED - straight], scalar1=-0.5,
+                                            scalar2=None, op0=ALU.mult)
 
 
         acc_pool = ctx.enter_context(tc.tile_pool(name="acc_pool", bufs=2))

@@ -28,8 +28,11 @@ JOB_BANKS = 3
 GROUP = 4
 BATCH = 32
 VECTOR_ROWS = 128
-FIRST_VECTOR_ROW = 1
-GPSIMD_ROWS = 24
+FIRST_VECTOR_ROW = 8
+GPSIMD_ROWS = 40
+G_LAG = 2
+ROW_SUM_WIDTH = 44
+FIRST_DUMMIES = 24
 SCALAR_JOB = 4
 EXP_LAG = 2
 LAST_ROWS = 12
@@ -40,7 +43,6 @@ EXP_BUFS = 8
 LAST_WIDTHS = [2, 2, 2, 1, 1]
 BIG = 3.0e38
 PLANE = EXT + GROUP
-SLANTED = GPSIMD_ROWS + GROUP + P
 HALF = IN_F // 2
 VECTOR_CLOSING = 3
 SCALAR_BANKS = [0, 1]
@@ -49,7 +51,7 @@ VECTOR_COLS = 384
 
 
 def first_column(m):
-    if m == ROWS:
+    if m >= ROWS:
         return m
     return m + 1
 
@@ -74,8 +76,9 @@ def tile_minibatchdiscriminator_kernel(tc, tensor, T_bytes, T_scale, out):
         make_identity(nc, ident[:])
         zeros = keep.tile([P, P], F32, name="zeros")
         nc.vector.memset(zeros[:], 0.0)
-        ones = keep.tile([P, 1], F32, name="ones")
-        nc.gpsimd.memset(ones[:], 1.0)
+        ones = keep.tile([P, ROW_SUM_WIDTH], F32, name="ones")
+        nc.gpsimd.memset(ones[:], 0.0)
+        nc.gpsimd.memset(ones[:, 0:1], 1.0)
         col_sums = keep.tile([P, GROUP, PLANE], F32, name="col_sums")
         nc.vector.memset(col_sums[:], 0.0)
         nc.vector.memset(col_sums[:, 0, GROUP - 1:GROUP - 1 + ROWS], 1.0)
@@ -84,12 +87,14 @@ def tile_minibatchdiscriminator_kernel(tc, tensor, T_bytes, T_scale, out):
         nc.vector.memset(row_sums[:], 0.0)
         totals_sb = keep.tile([P, EXT], F32, name="totals_sb")
         nc.vector.memset(totals_sb[:], 0.0)
+        extra_sb = keep.tile([P, P], F32, name="extra_sb")
+        nc.vector.memset(extra_sb[:], 0.0)
 
-        f_sw = keep.tile([P, KK, ROWS], F32, name="f_sw")
+        f_sw = keep.tile([P, KK, ROWS + FIRST_VECTOR_ROW], F32, name="f_sw")
         f_t = keep.tile([P, 2, KK, P], F32, name="f_t")
         s_sum = keep.tile([P, ROWS], F32, name="s_sum")
         minus_half_s = keep.tile([P, ROWS], F32, name="minus_half_s")
-        minus_half_s_slanted = keep.tile([P, GROUP, SLANTED], F32, name="minus_half_s_slanted")
+        minus_half_s_sw = keep.tile([P, ROWS], F32, name="minus_half_s_sw")
         f_bank = []
 
         def f_columns(k, c):
@@ -232,7 +237,7 @@ def tile_minibatchdiscriminator_kernel(tc, tensor, T_bytes, T_scale, out):
                     if q < RING:
                         moves = [(f_sw[:, 2 * q:2 * q + 2, P:ROWS], bank[:, :, 0:P]), (f_sw[:, 2 * q:2 * q + 2, 0:P], bank[:, :, P:ROWS])]
                     else:
-                        moves = [(f_sw[:, 2 * q:2 * q + 2, :], bank[:])]
+                        moves = [(f_sw[:, 2 * q:2 * q + 2, 0:ROWS], bank[:])]
                     for dst, part in moves:
                         if q in SCALAR_BANKS:
                             nc.scalar.copy(out=dst, in_=part)
@@ -245,23 +250,21 @@ def tile_minibatchdiscriminator_kernel(tc, tensor, T_bytes, T_scale, out):
                                          is_transpose=True)
                 nc.vector.tensor_scalar(out=minus_half_s[:], in0=s_bank[:], scalar1=-0.5, scalar2=None, op0=ALU.mult)
                 nc.vector.tensor_copy(out=s_sum[:], in_=s_bank[:])
-                for r in range(GROUP):
-                    straight = ROWS - VECTOR_ROWS - r
-                    nc.vector.tensor_scalar(out=minus_half_s_slanted[:, r, 0:straight], in0=s_bank[:, VECTOR_ROWS + r:ROWS], scalar1=-0.5,
-                                            scalar2=None, op0=ALU.mult)
-                    nc.vector.tensor_scalar(out=minus_half_s_slanted[:, r, straight:SLANTED], in0=s_bank[:, 0:SLANTED - straight], scalar1=-0.5,
-                                            scalar2=None, op0=ALU.mult)
+                nc.vector.tensor_scalar(out=minus_half_s_sw[:, 0:P], in0=s_bank[:, P:ROWS], scalar1=-0.5, scalar2=None, op0=ALU.mult)
+                nc.vector.tensor_scalar(out=minus_half_s_sw[:, P:ROWS], in0=s_bank[:, 0:P], scalar1=-0.5, scalar2=None, op0=ALU.mult)
 
 
         acc_pool = ctx.enter_context(tc.tile_pool(name="acc_pool", bufs=2))
         exp_pool = ctx.enter_context(tc.tile_pool(name="exp_pool", bufs=EXP_BUFS))
         term_pool = ctx.enter_context(tc.tile_pool(name="term_pool", bufs=TERM_BUFS))
-        own_pool = ctx.enter_context(tc.tile_pool(name="own_pool", bufs=2))
+        own_pool = ctx.enter_context(tc.tile_pool(name="own_pool", bufs=G_LAG + 2))
         turned_pool = ctx.enter_context(tc.tile_pool(name="turned_pool", bufs=3))
 
-        vector_groups = list(range(0, VECTOR_ROWS, GROUP))
+        vector_groups = list(range(FIRST_VECTOR_ROW, VECTOR_ROWS, GROUP))
         per_batch = BATCH // GROUP
-        batches = [vector_groups[i:i + per_batch] for i in range(0, len(vector_groups), per_batch)]
+        short = len(vector_groups) % per_batch
+        batches = [vector_groups[0:short]] if short else []
+        batches.extend([vector_groups[i:i + per_batch] for i in range(short, len(vector_groups), per_batch)])
         visits = []
         for b in range(len(batches)):
             visits.extend([(b, q if b % 2 == 0 else PAIRS - 1 - q) for q in range(PAIRS)])
@@ -275,29 +278,22 @@ def tile_minibatchdiscriminator_kernel(tc, tensor, T_bytes, T_scale, out):
             pieces_of.extend([(number, g0, g0 + width) for number in range(last_half, len(visits))])
             g0 += width
         vector_total = float(sum([g1 - g0 for number, g0, g1 in pieces_of]))
-        gpsimd_pieces = []
-        for m0 in range(VECTOR_ROWS, VECTOR_ROWS + GPSIMD_ROWS, GROUP):
-            n = min(GROUP, VECTOR_ROWS + GPSIMD_ROWS - m0)
-            gpsimd_pieces.extend([("row", m0 + r, 0, KK * P) for r in range(n)])
-            gpsimd_pieces.extend([("halve", n, half, n * half * P) for half in (8, 4, 2, 1)])
-            gpsimd_pieces.append(("last", m0, n, n * P))
-        gpsimd_total = float(sum([piece[3] for piece in gpsimd_pieces]))
+        gpsimd_pieces = list(range(VECTOR_ROWS, VECTOR_ROWS + GPSIMD_ROWS)) + [0] * G_LAG
         scalar_first = VECTOR_ROWS + GPSIMD_ROWS
         scalar_rows = list(range(scalar_first, ROWS + FIRST_VECTOR_ROW))
-        row_slot = EXT - scalar_first
-        rows_left = [len(scalar_rows)]
+        rows_left = [len(scalar_rows) + GPSIMD_ROWS]
 
         ring = {}
         for v in range(RING):
             ring[v] = f_bank[v]
         acc_of = {}
-        fresh = {0: [], 2: []}
+        fresh = []
         exps_due = []
         cols_due = []
         jobs = []
         open_job = []
         ready = []
-        own_terms = []
+        waiting = []
 
         def refill(v):
             b, q = visits[v]
@@ -318,13 +314,10 @@ def tile_minibatchdiscriminator_kernel(tc, tensor, T_bytes, T_scale, out):
                 acc_of[b] = acc_new
             acc = acc_of[b]
             for s in range(2):
-                k = 2 * q + s
                 for gi in range(g0, g1):
                     for r in range(GROUP):
                         row = gi * GROUP + r
                         m = batches[b][gi] + r
-                        if m < FIRST_VECTOR_ROW:
-                            continue
                         c = first_column(m)
                         w = window(m)
                         nc.vector.scalar_tensor_tensor(
@@ -337,12 +330,12 @@ def tile_minibatchdiscriminator_kernel(tc, tensor, T_bytes, T_scale, out):
                         )
             if v % PAIRS == PAIRS - 1:
                 for gi in range(g0, g1):
-                    first = max(batches[b][gi], FIRST_VECTOR_ROW)
-                    fresh[0].append((acc[:, gi * GROUP + first - batches[b][gi]:(gi + 1) * GROUP, 0:window(first)], first))
+                    first = batches[b][gi]
+                    fresh.append((acc[:, gi * GROUP:(gi + 1) * GROUP, 0:window(first)], first))
 
-        def release(route):
-            exps_due.extend([(sums, m0, i_s) for sums, m0 in fresh[route]])
-            fresh[route].clear()
+        def release():
+            exps_due.extend([(sums, m0, i_s) for sums, m0 in fresh])
+            fresh.clear()
 
         def group_exp(step):
             lag = EXP_LAG if i_s < len(scalar_rows) - LAST_ROWS else EXP_LAG - 1
@@ -372,53 +365,54 @@ def tile_minibatchdiscriminator_kernel(tc, tensor, T_bytes, T_scale, out):
                                      scale=-1.0)
             return [terms[:, k, :] for k in range(KK)]
 
-        def gpsimd_row(m):
-            r = (m - VECTOR_ROWS) % GROUP
-            if r == 0:
-                terms_new = own_pool.tile([P, GROUP, KK, P], F32, name="max_terms", tag="max_terms", bufs=1)
-                own_terms.clear()
-                own_terms.append(terms_new)
+        def gpsimd_terms(m):
+            terms = own_pool.tile([P, KK, P], F32, name="max_terms", tag="max_terms")
             c = first_column(m)
             for k in range(KK):
-                nc.gpsimd.tensor_scalar(out=own_terms[0][:, r, k, :], in0=f_columns(k, c), scalar1=BIG,
+                nc.gpsimd.tensor_scalar(out=terms[:, k, :], in0=f_columns(k, c), scalar1=BIG,
                                         scalar2=f_value(k, m), op0=ALU.min, op1=ALU.max)
-
-        def gpsimd_halve(n, half):
-            terms = own_terms[0]
-            nc.gpsimd.tensor_tensor(out=terms[:, 0:n, 0:half, :], in0=terms[:, 0:n, 0:half, :], in1=terms[:, 0:n, half:2 * half, :],
-                                    op=ALU.add)
-
-        def gpsimd_last(m0, n):
-            sums = own_pool.tile([P, GROUP, P], F32, name="own_sums", tag="own_sums")
-            c0 = first_column(m0) - VECTOR_ROWS
-            nc.gpsimd.tensor_tensor(out=sums[:, 0:n, :], in0=own_terms[0][:, 0:n, 0, :], in1=minus_half_s_slanted[:, 0:n, c0:c0 + P],
-                                    op=ALU.add)
-            fresh[2].append((sums[:, 0:n, :], m0))
+            pieces = [terms[:, k, :] for k in range(KK)]
+            pieces.append(minus_half_s_sw[:, c - P:c])
+            pieces.append(minus_half_s[:, m:m + 1].to_broadcast([P, P]))
+            return pieces
 
         def new_job():
             bank = psum.tile([P, SCALAR_JOB, P], F32, name="job", tag="bank%d" % (RING + (len(jobs) + 1) % JOB_BANKS))
-            job = [[], bank]
+            job = [[], bank, []]
             jobs.append(job)
             return job
 
-        def add_terms(job, m, pieces):
+        def hand_over(m, pieces, factor, close):
+            if not open_job:
+                open_job.append(new_job())
+            job = open_job[0]
             slot = len(job[0])
             job[0].append(m)
+            job[2].append(factor)
             for i, piece in enumerate(pieces):
                 nc.tensor.matmul(out=job[1][:, slot, :], lhsT=piece, rhs=ident[:], start=(i == 0), stop=(i == len(pieces) - 1),
                                  is_transpose=True)
+            if len(job[0]) == SCALAR_JOB or close:
+                ready.append((open_job.pop(0), i_s))
 
         def finish(job):
-            rows, bank = job
+            rows, bank, factors = job
             turned = turned_pool.tile([P, SCALAR_JOB, P], F32, name="turned", tag="turned")
-            nc.scalar.activation(out=turned[:, 0:len(rows), :], in_=bank[:, 0:len(rows), :], func=ACT.Exp, scale=-1.0)
+            first = 0
+            while first < len(rows):
+                end = first + 1
+                while end < len(rows) and factors[end] == factors[first]:
+                    end += 1
+                nc.scalar.activation(out=turned[:, first:end, :], in_=bank[:, first:end, :], func=ACT.Exp, scale=-factors[first])
+                first = end
             for slot, m in enumerate(rows):
-                c = first_column(m) - scalar_first
+                c = first_column(m) - VECTOR_ROWS
                 nc.tensor.matmul(out=totals[:, c:c + P], lhsT=turned[:, slot, :], rhs=ident[:], start=False, stop=False,
                                  is_transpose=True)
+            for slot, m in enumerate(rows):
                 rows_left[0] -= 1
-                i = m - scalar_first
-                nc.tensor.matmul(out=totals[:, i:i + 1], lhsT=turned[:, slot, :], rhs=ones[:],
+                i = m - VECTOR_ROWS
+                nc.tensor.matmul(out=totals[:, i:i + ROW_SUM_WIDTH], lhsT=turned[:, slot, :], rhs=ones[:],
                                  start=False, stop=(rows_left[0] == 0))
 
         def finish_ready(before):
@@ -429,7 +423,6 @@ def tile_minibatchdiscriminator_kernel(tc, tensor, T_bytes, T_scale, out):
         vector_done = 0
         i_s = 0
         i_g = 0
-        gpsimd_done = 0
         step = 0
 
         with tc.manual_schedule():
@@ -437,6 +430,8 @@ def tile_minibatchdiscriminator_kernel(tc, tensor, T_bytes, T_scale, out):
             for i in range(4):
                 nc.tensor.matmul(out=totals[:, i * P:(i + 1) * P], lhsT=zeros[:], rhs=ident[:], start=(i == 0), stop=False,
                                  is_transpose=True)
+            for i in range(FIRST_DUMMIES):
+                nc.tensor.matmul(out=totals[:, 0:P], lhsT=zeros[:], rhs=ident[:], start=False, stop=False, is_transpose=True)
             while i_v < len(pieces_of) or i_s < len(scalar_rows) or i_g < len(gpsimd_pieces):
                 shares = []
                 if i_v < len(pieces_of):
@@ -444,11 +439,11 @@ def tile_minibatchdiscriminator_kernel(tc, tensor, T_bytes, T_scale, out):
                 if i_s < len(scalar_rows):
                     shares.append((i_s / float(len(scalar_rows)), 1))
                 if i_g < len(gpsimd_pieces):
-                    shares.append((gpsimd_done / gpsimd_total * GPSIMD_AHEAD, 2))
+                    shares.append((i_g / float(len(gpsimd_pieces)) * GPSIMD_AHEAD, 2))
                 route = min(shares)[1]
                 step += 1
                 if route == 0:
-                    release(0)
+                    release()
                     v, g0, g1 = pieces_of[i_v]
                     vector_visit(v, g0, g1)
                     if g0 == 0 and RING <= v + 2 < len(visits):
@@ -457,50 +452,42 @@ def tile_minibatchdiscriminator_kernel(tc, tensor, T_bytes, T_scale, out):
                     i_v += 1
                 elif route == 1:
                     m = scalar_rows[i_s]
-                    pieces = scalar_terms(m)
-                    if not open_job:
-                        open_job.append(new_job())
-                    add_terms(open_job[0], m, pieces)
+                    hand_over(m, scalar_terms(m), 1.0, i_s >= len(scalar_rows) - 3)
                     group_exp(step)
                     finish_ready(i_s + 1 - JOB_LAG)
-                    if len(open_job[0][0]) == SCALAR_JOB or i_s >= len(scalar_rows) - 3:
-                        ready.append((open_job.pop(0), i_s))
                     i_s += 1
                 else:
-                    release(2)
-                    kind, first, second, elements = gpsimd_pieces[i_g]
-                    if kind == "row":
-                        gpsimd_row(first)
-                    elif kind == "halve":
-                        gpsimd_halve(first, second)
-                    else:
-                        gpsimd_last(first, second)
-                    gpsimd_done += elements
+                    if i_g < GPSIMD_ROWS:
+                        m = gpsimd_pieces[i_g]
+                        waiting.append((m, gpsimd_terms(m)))
+                        if i_g == 0:
+                            nc.gpsimd.tensor_copy(out=f_sw[:, :, ROWS:ROWS + FIRST_VECTOR_ROW], in_=f_sw[:, :, 0:FIRST_VECTOR_ROW])
+                    if i_g >= G_LAG:
+                        m, pieces = waiting.pop(0)
+                        hand_over(m, pieces, 2.0, False)
                     i_g += 1
-                if i_g == len(gpsimd_pieces):
-                    release(2)
                 if i_s == len(scalar_rows):
                     group_exp(step)
                     finish_ready(i_s)
                 add_columns(step - 1)
             step += 1
-            release(2)
-            release(0)
+            release()
             while exps_due:
                 group_exp(step)
-            finish_ready(i_s)
+            while open_job:
+                ready.append((open_job.pop(0), i_s))
+            finish_ready(i_s + 1)
             add_columns(step + 1)
 
-        nc.scalar.copy(out=totals_sb[:, ROWS:EXT], in_=totals[:, ROWS - scalar_first:EXT - scalar_first])
-        nc.vector.tensor_copy(out=totals_sb[:, scalar_first:ROWS], in_=totals[:, 0:ROWS - scalar_first])
+        nc.scalar.copy(out=totals_sb[:, ROWS:EXT], in_=totals[:, ROWS - VECTOR_ROWS:EXT - VECTOR_ROWS])
+        nc.vector.tensor_copy(out=totals_sb[:, VECTOR_ROWS:ROWS], in_=totals[:, 0:ROWS - VECTOR_ROWS])
+        nc.vector.tensor_copy(out=extra_sb[:, 0:FIRST_VECTOR_ROW], in_=totals[:, EXT - VECTOR_ROWS:EXT - VECTOR_ROWS + FIRST_VECTOR_ROW])
 
         diversity = []
         for h in range(2):
             half_sum = psum.tile([P, P], F32, name="diversity%d" % h, tag="bank%d" % h)
             diversity.append(half_sum)
-        parts = [(0, col_sums[:, r, GROUP - 1 - r + ROWS:GROUP - 1 - r + EXT]) for r in range(GROUP)]
-        parts.append((1, row_sums[:, P:ROWS]))
-        parts.append((0, row_sums[:, 0:P]))
+        parts = [(0, row_sums[:, 0:P])]
         for h in range(2):
             parts.extend([(h, col_sums[:, r, GROUP - 1 - r + h * P:GROUP - 1 - r + (h + 1) * P]) for r in range(GROUP)])
         opened = set()
@@ -510,6 +497,7 @@ def tile_minibatchdiscriminator_kernel(tc, tensor, T_bytes, T_scale, out):
         diversity_sb = keep.tile([P, 2, P], F32, name="diversity_sb")
         nc.tensor.matmul(out=diversity[0][:], lhsT=totals_sb[:, ROWS:EXT], rhs=ident[:], start=False, stop=True, is_transpose=True)
         nc.scalar.copy(out=diversity_sb[:, 0, :], in_=diversity[0][:])
+        nc.tensor.matmul(out=diversity[1][:], lhsT=extra_sb[:], rhs=ident[:], start=False, stop=False, is_transpose=True)
         nc.tensor.matmul(out=diversity[1][:], lhsT=totals_sb[:, P:ROWS], rhs=ident[:], start=False, stop=True, is_transpose=True)
         nc.vector.tensor_copy(out=diversity_sb[:, 1, :], in_=diversity[1][:])
         nc.sync.dma_start(out=out[:, IN_F:IN_F + P].rearrange("(h p) j -> p h j", p=P), in_=diversity_sb[:])

@@ -28,8 +28,8 @@ JOB_BANKS = 3
 GROUP = 4
 BATCH = 32
 VECTOR_ROWS = 128
-FIRST_VECTOR_ROW = 8
-GPSIMD_ROWS = 40
+FIRST_VECTOR_ROW = 10
+GPSIMD_ROWS = 41
 G_LAG = 2
 ROW_SUM_WIDTH = 44
 FIRST_DUMMIES = 24
@@ -260,7 +260,7 @@ def tile_minibatchdiscriminator_kernel(tc, tensor, T_bytes, T_scale, out):
         own_pool = ctx.enter_context(tc.tile_pool(name="own_pool", bufs=G_LAG + 2))
         turned_pool = ctx.enter_context(tc.tile_pool(name="turned_pool", bufs=3))
 
-        vector_groups = list(range(FIRST_VECTOR_ROW, VECTOR_ROWS, GROUP))
+        vector_groups = list(range(FIRST_VECTOR_ROW - FIRST_VECTOR_ROW % GROUP, VECTOR_ROWS, GROUP))
         per_batch = BATCH // GROUP
         short = len(vector_groups) % per_batch
         batches = [vector_groups[0:short]] if short else []
@@ -318,6 +318,8 @@ def tile_minibatchdiscriminator_kernel(tc, tensor, T_bytes, T_scale, out):
                     for r in range(GROUP):
                         row = gi * GROUP + r
                         m = batches[b][gi] + r
+                        if m < FIRST_VECTOR_ROW:
+                            continue
                         c = first_column(m)
                         w = window(m)
                         nc.vector.scalar_tensor_tensor(
@@ -330,8 +332,8 @@ def tile_minibatchdiscriminator_kernel(tc, tensor, T_bytes, T_scale, out):
                         )
             if v % PAIRS == PAIRS - 1:
                 for gi in range(g0, g1):
-                    first = batches[b][gi]
-                    fresh.append((acc[:, gi * GROUP:(gi + 1) * GROUP, 0:window(first)], first))
+                    first = max(batches[b][gi], FIRST_VECTOR_ROW)
+                    fresh.append((acc[:, gi * GROUP + first - batches[b][gi]:(gi + 1) * GROUP, 0:window(first)], first))
 
         def release():
             exps_due.extend([(sums, m0, i_s) for sums, m0 in fresh])

@@ -29,7 +29,7 @@ GROUP = 4
 BATCH = 32
 VECTOR_ROWS = 128
 FIRST_VECTOR_ROW = 10
-GPSIMD_ROWS = 41
+GPSIMD_ROWS = 40
 G_LAG = 2
 ROW_SUM_WIDTH = 44
 FIRST_DUMMIES = 24

@@ -31,7 +31,7 @@ VECTOR_ROWS = 128
 FIRST_VECTOR_ROW = 10
 GPSIMD_ROWS = 40
 G_LAG = 2
-ROW_SUM_WIDTH = 44
+ROW_SUM_WIDTH = 47
 FIRST_DUMMIES = 24
 SCALAR_JOB = 4
 EXP_LAG = 2
@@ -258,7 +258,7 @@ def tile_minibatchdiscriminator_kernel(tc, tensor, T_bytes, T_scale, out):
         exp_pool = ctx.enter_context(tc.tile_pool(name="exp_pool", bufs=EXP_BUFS))
         term_pool = ctx.enter_context(tc.tile_pool(name="term_pool", bufs=TERM_BUFS))
         own_pool = ctx.enter_context(tc.tile_pool(name="own_pool", bufs=G_LAG + 2))
-        turned_pool = ctx.enter_context(tc.tile_pool(name="turned_pool", bufs=3))
+        turned_pool = ctx.enter_context(tc.tile_pool(name="turned_pool", bufs=4))
 
         vector_groups = list(range(FIRST_VECTOR_ROW - FIRST_VECTOR_ROW % GROUP, VECTOR_ROWS, GROUP))
         per_batch = BATCH // GROUP
@@ -294,6 +294,7 @@ def tile_minibatchdiscriminator_kernel(tc, tensor, T_bytes, T_scale, out):
         open_job = []
         ready = []
         waiting = []
+        sums_due = []
 
         def refill(v):
             b, q = visits[v]
@@ -396,6 +397,7 @@ def tile_minibatchdiscriminator_kernel(tc, tensor, T_bytes, T_scale, out):
                                  is_transpose=True)
             if len(job[0]) == SCALAR_JOB or close:
                 ready.append((open_job.pop(0), i_s))
+            one_sum()
 
         def finish(job):
             rows, bank, factors = job
@@ -407,15 +409,16 @@ def tile_minibatchdiscriminator_kernel(tc, tensor, T_bytes, T_scale, out):
                     end += 1
                 nc.scalar.activation(out=turned[:, first:end, :], in_=bank[:, first:end, :], func=ACT.Exp, scale=-factors[first])
                 first = end
-            for slot, m in enumerate(rows):
+            sums_due.extend([(turned[:, slot, :], m) for slot, m in enumerate(rows)])
+
+        def one_sum():
+            if sums_due:
+                exps, m = sums_due.pop(0)
                 c = first_column(m) - VECTOR_ROWS
-                nc.tensor.matmul(out=totals[:, c:c + P], lhsT=turned[:, slot, :], rhs=ident[:], start=False, stop=False,
-                                 is_transpose=True)
-            for slot, m in enumerate(rows):
+                nc.tensor.matmul(out=totals[:, c:c + P], lhsT=exps, rhs=ident[:], start=False, stop=False, is_transpose=True)
                 rows_left[0] -= 1
                 i = m - VECTOR_ROWS
-                nc.tensor.matmul(out=totals[:, i:i + ROW_SUM_WIDTH], lhsT=turned[:, slot, :], rhs=ones[:],
-                                 start=False, stop=(rows_left[0] == 0))
+                nc.tensor.matmul(out=totals[:, i:i + ROW_SUM_WIDTH], lhsT=exps, rhs=ones[:], start=False, stop=(rows_left[0] == 0))
 
         def finish_ready(before):
             while ready and ready[0][1] < before:
@@ -479,6 +482,8 @@ def tile_minibatchdiscriminator_kernel(tc, tensor, T_bytes, T_scale, out):
             while open_job:
                 ready.append((open_job.pop(0), i_s))
             finish_ready(i_s + 1)
+            while sums_due:
+                one_sum()
             add_columns(step + 1)
 
         nc.scalar.copy(out=totals_sb[:, ROWS:EXT], in_=totals[:, ROWS - VECTOR_ROWS:EXT - VECTOR_ROWS])

@@ -28,7 +28,8 @@ JOB_BANKS = 3
 GROUP = 4
 BATCH = 32
 VECTOR_ROWS = 128
-FIRST_VECTOR_ROW = 10
+FIRST_VECTOR_ROW = 9
+SCALAR_AHEAD = 0.98
 GPSIMD_ROWS = 40
 G_LAG = 2
 ROW_SUM_WIDTH = 47
@@ -442,7 +443,7 @@ def tile_minibatchdiscriminator_kernel(tc, tensor, T_bytes, T_scale, out):
                 if i_v < len(pieces_of):
                     shares.append((vector_done / vector_total, 0))
                 if i_s < len(scalar_rows):
-                    shares.append((i_s / float(len(scalar_rows)), 1))
+                    shares.append((i_s / float(len(scalar_rows)) * SCALAR_AHEAD, 1))
                 if i_g < len(gpsimd_pieces):
                     shares.append((i_g / float(len(gpsimd_pieces)) * GPSIMD_AHEAD, 2))
                 route = min(shares)[1]

@@ -28,10 +28,10 @@ JOB_BANKS = 3
 GROUP = 4
 BATCH = 32
 VECTOR_ROWS = 128
-FIRST_VECTOR_ROW = 9
+FIRST_VECTOR_ROW = 10
 SCALAR_AHEAD = 0.98
-GPSIMD_ROWS = 40
-G_LAG = 2
+GPSIMD_ROWS = 41
+G_LAG = 3
 ROW_SUM_WIDTH = 47
 FIRST_DUMMIES = 24
 SCALAR_JOB = 4

@@ -28,7 +28,7 @@ JOB_BANKS = 3
 GROUP = 4
 BATCH = 32
 VECTOR_ROWS = 128
-FIRST_VECTOR_ROW = 10
+FIRST_VECTOR_ROW = 9
 SCALAR_AHEAD = 0.98
 GPSIMD_ROWS = 41
 G_LAG = 3

from contextlib import ExitStack

import concourse.mybir as mybir
from concourse.masks import make_identity

FLOPS = 2 * 256 * 2048 * 2048

F32 = mybir.dt.float32
BF16 = mybir.dt.bfloat16
U32 = mybir.dt.uint32
U8 = mybir.dt.uint8
FP8 = mybir.dt.float8_e4m3fn
FP8X4 = mybir.dt.float8_e4m3fn_x4
ALU = mybir.AluOpType
ACT = mybir.ActivationFunctionType
AX = mybir.AxisListType

P = 128
ROWS = 256
EXT = ROWS + P
IN_F = 2048
PACK = 4
PASSES = IN_F // (P * PACK)
KK = 16
PAIRS = KK // 2
RING = 4
JOB_BANKS = 3
GROUP = 4
BATCH = 32
VECTOR_ROWS = 128
FIRST_VECTOR_ROW = 9
SCALAR_AHEAD = 0.98
GPSIMD_ROWS = 41
G_LAG = 3
ROW_SUM_WIDTH = 47
FIRST_DUMMIES = 24
SCALAR_JOB = 4
EXP_LAG = 2
LAST_ROWS = 12
GPSIMD_AHEAD = 0.98
JOB_LAG = 3
TERM_BUFS = 6
EXP_BUFS = 8
LAST_WIDTHS = [2, 2, 2, 1, 1]
BIG = 3.0e38
PLANE = EXT + GROUP
HALF = IN_F // 2
VECTOR_CLOSING = 3
SCALAR_BANKS = [0, 1]
X_ON_VECTOR = []
VECTOR_COLS = 384


def first_column(m):
    if m >= ROWS:
        return m
    return m + 1


def window(m):
    if m < P:
        return P - 1
    return P


def tile_minibatchdiscriminator_kernel(tc, tensor, T_bytes, T_scale, out):
    nc = tc.nc
    with ExitStack() as ctx:
        keep = ctx.enter_context(tc.tile_pool(name="keep", bufs=1))
        psum = ctx.enter_context(tc.psum_pool(name="psum", bufs=1))

        warm = keep.tile([P, 2], F32, name="warm")
        nc.vector.memset(warm[:], 0.0)
        nc.scalar.activation(out=warm[:, 1:2], in_=warm[:, 0:1], func=ACT.Exp)

        ident = keep.tile([P, P], F32, name="ident")
        make_identity(nc, ident[:])
        zeros = keep.tile([P, P], F32, name="zeros")
        nc.vector.memset(zeros[:], 0.0)
        ones = keep.tile([P, ROW_SUM_WIDTH], F32, name="ones")
        nc.gpsimd.memset(ones[:], 0.0)
        nc.gpsimd.memset(ones[:, 0:1], 1.0)
        col_sums = keep.tile([P, GROUP, PLANE], F32, name="col_sums")
        nc.vector.memset(col_sums[:], 0.0)
        nc.vector.memset(col_sums[:, 0, GROUP - 1:GROUP - 1 + ROWS], 1.0)
        nc.vector.memset(col_sums[:, 0, GROUP - 1:GROUP - 1 + FIRST_VECTOR_ROW], -1.0)
        row_sums = keep.tile([P, ROWS], F32, name="row_sums")
        nc.vector.memset(row_sums[:], 0.0)
        totals_sb = keep.tile([P, EXT], F32, name="totals_sb")
        nc.vector.memset(totals_sb[:], 0.0)
        extra_sb = keep.tile([P, P], F32, name="extra_sb")
        nc.vector.memset(extra_sb[:], 0.0)

        f_sw = keep.tile([P, KK, ROWS + FIRST_VECTOR_ROW], F32, name="f_sw")
        f_t = keep.tile([P, 2, KK, P], F32, name="f_t")
        s_sum = keep.tile([P, ROWS], F32, name="s_sum")
        minus_half_s = keep.tile([P, ROWS], F32, name="minus_half_s")
        minus_half_s_sw = keep.tile([P, ROWS], F32, name="minus_half_s_sw")
        f_bank = []

        def f_columns(k, c):
            return f_sw[:, k, c - P:c]

        def f_value(k, m):
            place = (m + P) % ROWS
            return f_sw[:, k, place:place + 1]

        with ExitStack() as head:
            bytes_pool = head.enter_context(tc.tile_pool(name="bytes_pool", bufs=1))
            stage = head.enter_context(tc.tile_pool(name="stage", bufs=2))
            mxp = head.enter_context(tc.tile_pool(name="mxp", bufs=1))

            t_scale = mxp.tile([P, PASSES, PACK], F32, name="t_scale")
            nc.scalar.dma_start(out=t_scale[:], in_=T_scale.rearrange("(g p t) a b -> p g (t a b)", p=P, t=PACK))
            bytes_view = T_bytes.rearrange("(g p t) j k -> g p (t j k)", p=P, t=PACK)
            x_sb = keep.tile([P, 2, IN_F], BF16, name="x_sb")
            t_bytes = []
            for g in range(PASSES):
                tb = bytes_pool.tile([P, PACK * IN_F], U8, name="t_bytes%d" % g)
                pieces = PACK if g == 0 else 2
                for piece in range(pieces):
                    run = slice(piece * PACK * IN_F // pieces, (piece + 1) * PACK * IN_F // pieces)
                    nc.sync.dma_start(out=tb[:, run], in_=bytes_view[g][:, run])
                    if g == 0:
                        x_cols = slice(piece * P * PACK, (piece + 1) * P * PACK)
                        nc.sync.dma_start(out=x_sb[:, :, x_cols], in_=tensor.rearrange("(h p) i -> p h i", p=P)[:, :, x_cols])
                t_bytes.append(tb)

            x_f32 = keep.tile([P, 2, IN_F], F32, name="x_f32")
            out_x = out[:, 0:IN_F].rearrange("(h p) i -> p h i", p=P)
            x_grouped = mxp.tile([P, PASSES, ROWS * PACK], BF16, name="x_grouped", align_bytes=64)
            x_codes = mxp.tile([P, PASSES * ROWS], U32, name="x_codes", align_bytes=64)
            x_scales = mxp.tile([P, PASSES * ROWS], U8, name="x_scales", align_bytes=64)
            t_codes = mxp.tile([P, PASSES, IN_F], U32, name="t_codes", align_bytes=64)
            t_scales = mxp.tile([P, PASSES, IN_F], U8, name="t_scales", align_bytes=64)
            widened = {}
            grouped_of = {}
            ft_bank = {}

            def widen(g):
                w = stage.tile([P, PACK, IN_F], BF16, name="w", tag="w")
                widened[g] = w
                for t in range(PACK):
                    nc.vector.tensor_scalar(out=w[:, t, :], in0=t_bytes[g][:, t * IN_F:(t + 1) * IN_F].bitcast(FP8),
                                            scalar1=t_scale[:, g, t:t + 1], scalar2=None, op0=ALU.mult)

            def interleave(g, half, c0, c1, on_scalar):
                dst = grouped_of[(g, half)][:, c0 * PACK:c1 * PACK].rearrange("p (c i t) -> p c t i", i=4, t=PACK)
                src = widened[g][:, :, half * HALF + c0:half * HALF + c1].rearrange("p t (c i) -> p c t i", i=4)
                if on_scalar:
                    nc.scalar.copy(out=dst, in_=src)
                else:
                    nc.vector.tensor_copy(out=dst, in_=src)

            def quantize(g, half):
                cols = slice(half * HALF, (half + 1) * HALF)
                nc.vector.quantize_mx(out=t_codes[:, g, cols].bitcast(FP8X4), scales=t_scales[:, g, cols],
                                      in_=grouped_of[(g, half)][:])

            def multiply(g, half):
                for cb in (2 * half, 2 * half + 1):
                    for h in range(2):
                        cols = slice(cb * 512, (cb + 1) * 512)
                        x_cols = slice(g * ROWS + h * P, g * ROWS + (h + 1) * P)
                        nc.tensor.matmul_mx(
                            out=ft_bank[(h, cb)][:],
                            lhsT=x_codes[:, x_cols].bitcast(FP8X4),
                            lhsT_scale=x_scales[:, x_cols],
                            rhs=t_codes[:, g, cols].bitcast(FP8X4),
                            rhs_scale=t_scales[:, g, cols],
                            start=(g == 0),
                            stop=(g == PASSES - 1),
                        )

            with tc.manual_schedule():
                widen(0)
                for g in range(PASSES):
                    x_t = psum.tile([P, 2, 2, P], F32, name="x_t%d" % g, tag="bank%d" % g)
                    for h in range(2):
                        words = x_sb[:, h, :].bitcast(F32)
                        for u in range(2):
                            nc.tensor.transpose(x_t[:, h, u, :], words[:, 256 * g + u:256 * (g + 1):2], ident[:])
                    x_dst = x_grouped[:, g, :].bitcast(F32).rearrange("p (h r u) -> p h r u", h=2, u=2)
                    if g in X_ON_VECTOR:
                        nc.vector.tensor_copy(out=x_dst, in_=x_t[:].rearrange("p h u r -> p h r u"))
                    else:
                        nc.scalar.copy(out=x_dst, in_=x_t[:].rearrange("p h u r -> p h r u"))
                for h in range(2):
                    for cb in range(4):
                        bank = psum.tile([P, 512], F32, name="ft_bank%d" % (4 * h + cb), tag="bank%d" % (4 * h + cb))
                        ft_bank[(h, cb)] = bank
                for g in range(PASSES):
                    last = g == PASSES - 1
                    for half in range(2):
                        t_grouped = stage.tile([P, HALF * PACK], BF16, name="t_grouped", tag="t_grouped", bufs=4, align_bytes=64)
                        grouped_of[(g, half)] = t_grouped
                    interleave(g, 0, 0, HALF, True)
                    if last:
                        interleave(g, 1, 0, HALF, False)
                    else:
                        interleave(g, 1, VECTOR_COLS, HALF, True)
                        interleave(g, 1, 0, VECTOR_COLS, False)
                    if g == 0:
                        nc.vector.quantize_mx(out=x_codes[:].bitcast(FP8X4), scales=x_scales[:],
                                              in_=x_grouped[:].rearrange("p g c -> p (g c)"))
                    else:
                        for half in range(2):
                            quantize(g - 1, half)
                            multiply(g - 1, half)
                    if not last:
                        widen(g + 1)
                for half in (1, 0):
                    quantize(PASSES - 1, half)
                    multiply(PASSES - 1, half)
                closing = [(h, cb) for cb in (2, 3, 0, 1) for h in range(2)]

                def cast(h):
                    nc.vector.tensor_copy(out=x_f32[:, h, :], in_=x_sb[:, h, :])
                    nc.sync.dma_start(out=out_x[:, h, :], in_=x_f32[:, h, :])

                cast(0)
                for i, (h, cb) in enumerate(closing):
                    dst = f_t[:, h, :, cb * 32:(cb + 1) * 32]
                    src = ft_bank[(h, cb)][:].rearrange("p (j k) -> p k j", k=KK)
                    if i < len(closing) - VECTOR_CLOSING:
                        nc.scalar.copy(out=dst, in_=src)
                    else:
                        nc.vector.tensor_copy(out=dst, in_=src)

                cast(1)
                for q in range(PAIRS):
                    bank = psum.tile([P, 2, ROWS], F32, name="f_bank%d" % q, tag="bank%d" % q)
                    f_bank.append(bank)
                    for s in range(2):
                        for h in range(2):
                            half = h if q < RING else 1 - h
                            nc.tensor.transpose(bank[:, s, half * P:(half + 1) * P], f_t[:, h, 2 * q + s, :], ident[:])
                    if q < RING:
                        moves = [(f_sw[:, 2 * q:2 * q + 2, P:ROWS], bank[:, :, 0:P]), (f_sw[:, 2 * q:2 * q + 2, 0:P], bank[:, :, P:ROWS])]
                    else:
                        moves = [(f_sw[:, 2 * q:2 * q + 2, 0:ROWS], bank[:])]
                    for dst, part in moves:
                        if q in SCALAR_BANKS:
                            nc.scalar.copy(out=dst, in_=part)
                        else:
                            nc.vector.tensor_copy(out=dst, in_=part)
                s_bank = psum.tile([P, ROWS], F32, name="s_bank", tag="bank%d" % RING)
                for h in range(2):
                    for k in range(KK):
                        nc.tensor.matmul(out=s_bank[:, h * P:(h + 1) * P], lhsT=f_t[:, h, k, :], rhs=ident[:], start=(k == 0), stop=(k == KK - 1),
                                         is_transpose=True)
                nc.vector.tensor_scalar(out=minus_half_s[:], in0=s_bank[:], scalar1=-0.5, scalar2=None, op0=ALU.mult)
                nc.vector.tensor_copy(out=s_sum[:], in_=s_bank[:])
                nc.vector.tensor_scalar(out=minus_half_s_sw[:, 0:P], in0=s_bank[:, P:ROWS], scalar1=-0.5, scalar2=None, op0=ALU.mult)
                nc.vector.tensor_scalar(out=minus_half_s_sw[:, P:ROWS], in0=s_bank[:, 0:P], scalar1=-0.5, scalar2=None, op0=ALU.mult)


        acc_pool = ctx.enter_context(tc.tile_pool(name="acc_pool", bufs=2))
        exp_pool = ctx.enter_context(tc.tile_pool(name="exp_pool", bufs=EXP_BUFS))
        term_pool = ctx.enter_context(tc.tile_pool(name="term_pool", bufs=TERM_BUFS))
        own_pool = ctx.enter_context(tc.tile_pool(name="own_pool", bufs=G_LAG + 2))
        turned_pool = ctx.enter_context(tc.tile_pool(name="turned_pool", bufs=4))

        vector_groups = list(range(FIRST_VECTOR_ROW - FIRST_VECTOR_ROW % GROUP, VECTOR_ROWS, GROUP))
        per_batch = BATCH // GROUP
        short = len(vector_groups) % per_batch
        batches = [vector_groups[0:short]] if short else []
        batches.extend([vector_groups[i:i + per_batch] for i in range(short, len(vector_groups), per_batch)])
        visits = []
        for b in range(len(batches)):
            visits.extend([(b, q if b % 2 == 0 else PAIRS - 1 - q) for q in range(PAIRS)])
        pieces_of = []
        last_half = len(visits) - RING
        for number, (b, q) in enumerate(visits[0:last_half]):
            width = 2 if number % PAIRS == PAIRS - 1 else len(batches[b])
            pieces_of.extend([(number, g0, min(g0 + width, len(batches[b]))) for g0 in range(0, len(batches[b]), width)])
        g0 = 0
        for width in LAST_WIDTHS:
            pieces_of.extend([(number, g0, g0 + width) for number in range(last_half, len(visits))])
            g0 += width
        vector_total = float(sum([g1 - g0 for number, g0, g1 in pieces_of]))
        gpsimd_pieces = list(range(VECTOR_ROWS, VECTOR_ROWS + GPSIMD_ROWS)) + [0] * G_LAG
        scalar_first = VECTOR_ROWS + GPSIMD_ROWS
        scalar_rows = list(range(scalar_first, ROWS + FIRST_VECTOR_ROW))
        rows_left = [len(scalar_rows) + GPSIMD_ROWS]

        ring = {}
        for v in range(RING):
            ring[v] = f_bank[v]
        acc_of = {}
        fresh = []
        exps_due = []
        cols_due = []
        jobs = []
        open_job = []
        ready = []
        waiting = []
        sums_due = []

        def refill(v):
            b, q = visits[v]
            place = v % PAIRS
            if place < RING:
                ring[v] = ring[v - 1 - 2 * place]
                return
            bank = psum.tile([P, 2, ROWS], F32, name="ring", tag="bank%d" % (place % RING if b % 2 == 0 else RING - 1 - place % RING))
            for s in range(2):
                for h in range(2):
                    nc.tensor.transpose(bank[:, s, h * P:(h + 1) * P], f_t[:, h, 2 * q + s, :], ident[:])
            ring[v] = bank

        def vector_visit(v, g0, g1):
            b, q = visits[v]
            if v % PAIRS == 0:
                acc_new = acc_pool.tile([P, BATCH, P], F32, name="acc", tag="acc")
                acc_of[b] = acc_new
            acc = acc_of[b]
            for s in range(2):
                for gi in range(g0, g1):
                    for r in range(GROUP):
                        row = gi * GROUP + r
                        m = batches[b][gi] + r
                        if m < FIRST_VECTOR_ROW:
                            continue
                        c = first_column(m)
                        w = window(m)
                        nc.vector.scalar_tensor_tensor(
                            out=acc[:, row, 0:w],
                            in0=ring[v][:, s, c:c + w],
                            scalar=ring[v][:, s, m:m + 1],
                            in1=(minus_half_s[:, c:c + w] if v % PAIRS == 0 and s == 0 else acc[:, row, 0:w]),
                            op0=ALU.max,
                            op1=ALU.add,
                        )
            if v % PAIRS == PAIRS - 1:
                for gi in range(g0, g1):
                    first = max(batches[b][gi], FIRST_VECTOR_ROW)
                    fresh.append((acc[:, gi * GROUP + first - batches[b][gi]:(gi + 1) * GROUP, 0:window(first)], first))

        def release():
            exps_due.extend([(sums, m0, i_s) for sums, m0 in fresh])
            fresh.clear()

        def group_exp(step):
            lag = EXP_LAG if i_s < len(scalar_rows) - LAST_ROWS else EXP_LAG - 1
            if exps_due and (exps_due[0][2] + lag <= i_s or i_s >= len(scalar_rows) - 1):
                sums, m0, since = exps_due.pop(0)
                e = exp_pool.tile([P, GROUP, P], F32, name="e", tag="e")
                for r in range(sums.shape[1]):
                    m = m0 + r
                    nc.scalar.activation(out=e[:, r, 0:window(m)], in_=sums[:, r, :], func=ACT.Exp, bias=s_sum[:, m:m + 1], scale=-2.0,
                                         accum_out=row_sums[:, m:m + 1])
                cols_due.append((e[:, 0:sums.shape[1], 0:window(m0)], m0, step))

        def add_columns(before):
            while cols_due and cols_due[0][2] < before:
                e, m0, issued = cols_due.pop(0)
                target = col_sums[:, 0:e.shape[1], m0 + GROUP:m0 + GROUP + e.shape[2]]
                if m0 == VECTOR_ROWS - GROUP:
                    nc.vector.tensor_tensor(out=target, in0=target, in1=e, op=ALU.add)
                else:
                    nc.gpsimd.tensor_tensor(out=target, in0=target, in1=e, op=ALU.add)

        def scalar_terms(m):
            terms = term_pool.tile([P, KK, P], F32, name="abs_terms", tag="abs_terms")
            c = first_column(m)
            for k in range(KK):
                nc.scalar.activation(out=terms[:, k, :], in_=f_columns(k, c), func=ACT.Abs, bias=f_value(k, m),
                                     scale=-1.0)
            return [terms[:, k, :] for k in range(KK)]

        def gpsimd_terms(m):
            terms = own_pool.tile([P, KK, P], F32, name="max_terms", tag="max_terms")
            c = first_column(m)
            for k in range(KK):
                nc.gpsimd.tensor_scalar(out=terms[:, k, :], in0=f_columns(k, c), scalar1=BIG,
                                        scalar2=f_value(k, m), op0=ALU.min, op1=ALU.max)
            pieces = [terms[:, k, :] for k in range(KK)]
            pieces.append(minus_half_s_sw[:, c - P:c])
            pieces.append(minus_half_s[:, m:m + 1].to_broadcast([P, P]))
            return pieces

        def new_job():
            bank = psum.tile([P, SCALAR_JOB, P], F32, name="job", tag="bank%d" % (RING + (len(jobs) + 1) % JOB_BANKS))
            job = [[], bank, []]
            jobs.append(job)
            return job

        def hand_over(m, pieces, factor, close):
            if not open_job:
                open_job.append(new_job())
            job = open_job[0]
            slot = len(job[0])
            job[0].append(m)
            job[2].append(factor)
            for i, piece in enumerate(pieces):
                nc.tensor.matmul(out=job[1][:, slot, :], lhsT=piece, rhs=ident[:], start=(i == 0), stop=(i == len(pieces) - 1),
                                 is_transpose=True)
            if len(job[0]) == SCALAR_JOB or close:
                ready.append((open_job.pop(0), i_s))
            one_sum()

        def finish(job):
            rows, bank, factors = job
            turned = turned_pool.tile([P, SCALAR_JOB, P], F32, name="turned", tag="turned")
            first = 0
            while first < len(rows):
                end = first + 1
                while end < len(rows) and factors[end] == factors[first]:
                    end += 1
                nc.scalar.activation(out=turned[:, first:end, :], in_=bank[:, first:end, :], func=ACT.Exp, scale=-factors[first])
                first = end
            sums_due.extend([(turned[:, slot, :], m) for slot, m in enumerate(rows)])

        def one_sum():
            if sums_due:
                exps, m = sums_due.pop(0)
                c = first_column(m) - VECTOR_ROWS
                nc.tensor.matmul(out=totals[:, c:c + P], lhsT=exps, rhs=ident[:], start=False, stop=False, is_transpose=True)
                rows_left[0] -= 1
                i = m - VECTOR_ROWS
                nc.tensor.matmul(out=totals[:, i:i + ROW_SUM_WIDTH], lhsT=exps, rhs=ones[:], start=False, stop=(rows_left[0] == 0))

        def finish_ready(before):
            while ready and ready[0][1] < before:
                finish(ready.pop(0)[0])

        i_v = 0
        vector_done = 0
        i_s = 0
        i_g = 0
        step = 0

        with tc.manual_schedule():
            totals = psum.tile([P, 4 * P], F32, name="totals", tag="bank%d" % (RING + JOB_BANKS))
            for i in range(4):
                nc.tensor.matmul(out=totals[:, i * P:(i + 1) * P], lhsT=zeros[:], rhs=ident[:], start=(i == 0), stop=False,
                                 is_transpose=True)
            for i in range(FIRST_DUMMIES):
                nc.tensor.matmul(out=totals[:, 0:P], lhsT=zeros[:], rhs=ident[:], start=False, stop=False, is_transpose=True)
            while i_v < len(pieces_of) or i_s < len(scalar_rows) or i_g < len(gpsimd_pieces):
                shares = []
                if i_v < len(pieces_of):
                    shares.append((vector_done / vector_total, 0))
                if i_s < len(scalar_rows):
                    shares.append((i_s / float(len(scalar_rows)) * SCALAR_AHEAD, 1))
                if i_g < len(gpsimd_pieces):
                    shares.append((i_g / float(len(gpsimd_pieces)) * GPSIMD_AHEAD, 2))
                route = min(shares)[1]
                step += 1
                if route == 0:
                    release()
                    v, g0, g1 = pieces_of[i_v]
                    vector_visit(v, g0, g1)
                    if g0 == 0 and RING <= v + 2 < len(visits):
                        refill(v + 2)
                    vector_done += g1 - g0
                    i_v += 1
                elif route == 1:
                    m = scalar_rows[i_s]
                    hand_over(m, scalar_terms(m), 1.0, i_s >= len(scalar_rows) - 3)
                    group_exp(step)
                    finish_ready(i_s + 1 - JOB_LAG)
                    i_s += 1
                else:
                    if i_g < GPSIMD_ROWS:
                        m = gpsimd_pieces[i_g]
                        waiting.append((m, gpsimd_terms(m)))
                        if i_g == 0:
                            nc.gpsimd.tensor_copy(out=f_sw[:, :, ROWS:ROWS + FIRST_VECTOR_ROW], in_=f_sw[:, :, 0:FIRST_VECTOR_ROW])
                    if i_g >= G_LAG:
                        m, pieces = waiting.pop(0)
                        hand_over(m, pieces, 2.0, False)
                    i_g += 1
                if i_s == len(scalar_rows):
                    group_exp(step)
                    finish_ready(i_s)
                add_columns(step - 1)
            step += 1
            release()
            while exps_due:
                group_exp(step)
            while open_job:
                ready.append((open_job.pop(0), i_s))
            finish_ready(i_s + 1)
            while sums_due:
                one_sum()
            add_columns(step + 1)

        nc.scalar.copy(out=totals_sb[:, ROWS:EXT], in_=totals[:, ROWS - VECTOR_ROWS:EXT - VECTOR_ROWS])
        nc.vector.tensor_copy(out=totals_sb[:, VECTOR_ROWS:ROWS], in_=totals[:, 0:ROWS - VECTOR_ROWS])
        nc.vector.tensor_copy(out=extra_sb[:, 0:FIRST_VECTOR_ROW], in_=totals[:, EXT - VECTOR_ROWS:EXT - VECTOR_ROWS + FIRST_VECTOR_ROW])

        diversity = []
        for h in range(2):
            half_sum = psum.tile([P, P], F32, name="diversity%d" % h, tag="bank%d" % h)
            diversity.append(half_sum)
        parts = [(0, row_sums[:, 0:P])]
        for h in range(2):
            parts.extend([(h, col_sums[:, r, GROUP - 1 - r + h * P:GROUP - 1 - r + (h + 1) * P]) for r in range(GROUP)])
        opened = set()
        for h, part in parts:
            nc.tensor.matmul(out=diversity[h][:], lhsT=part, rhs=ident[:], start=(h not in opened), stop=False, is_transpose=True)
            opened.add(h)
        diversity_sb = keep.tile([P, 2, P], F32, name="diversity_sb")
        nc.tensor.matmul(out=diversity[0][:], lhsT=totals_sb[:, ROWS:EXT], rhs=ident[:], start=False, stop=True, is_transpose=True)
        nc.scalar.copy(out=diversity_sb[:, 0, :], in_=diversity[0][:])
        nc.tensor.matmul(out=diversity[1][:], lhsT=extra_sb[:], rhs=ident[:], start=False, stop=False, is_transpose=True)
        nc.tensor.matmul(out=diversity[1][:], lhsT=totals_sb[:, P:ROWS], rhs=ident[:], start=False, stop=True, is_transpose=True)
        nc.vector.tensor_copy(out=diversity_sb[:, 1, :], in_=diversity[1][:])
        nc.sync.dma_start(out=out[:, IN_F:IN_F + P].rearrange("(h p) j -> p h j", p=P), in_=diversity_sb[:])
